import numpy as np
import ml_dtypes


def mxq(x, axis, fmt="e4m3"):
    dtype, down = {"e4m3": (ml_dtypes.float8_e4m3fn, 7), "e5m2": (ml_dtypes.float8_e5m2, 14)}[fmt]
    v = np.moveaxis(np.asarray(x, np.float32).astype(ml_dtypes.bfloat16).astype(np.float64), axis, -1)
    blocks = v.reshape(v.shape[:-1] + (-1, 32))
    amax = np.abs(blocks).max(-1, keepdims=True)
    byte = np.maximum(np.where(amax > 0, np.frexp(amax)[1] - 1 + 127, 0) - down, 1)
    scale = np.exp2(byte - 127.0)
    codes = (blocks / scale).astype(np.float32).astype(dtype).astype(np.float64)
    return np.moveaxis((codes * scale).reshape(v.shape), -1, axis)


WIDE = False


def mx_kscale(k):
    if not WIDE:
        return np.ones(k)
    levels = np.array([10, -10, 5, -5, 0])
    a = np.random.permutation(np.resize(levels, k // 512 * 4)).reshape(k // 512, 4)
    idx = np.arange(k)
    return np.exp2(a[idx // 512, idx % 128 // 32])


BF16 = ml_dtypes.bfloat16


def bf(x):
    return np.asarray(x, np.float32).astype(BF16)


def f64(x):
    return np.asarray(x).astype(np.float64)


B, S, E, H = 4, 2048, 512, 4
D = E // H
LN_EPS = 1e-6


def setup_inputs():
    s = mx_kscale(E)
    return {"h_attn": bf(np.random.standard_normal((B, H, S, D)) * 0.4 * s.reshape(H, 1, D)),
            "x": bf(np.random.standard_normal((B, S, E))),
            "out_w": bf(np.random.standard_normal((E, E)) * 2.0 / np.sqrt(E) / s[:, None]),
            "ln_gamma": bf(1.0 + 0.1 * np.random.standard_normal(E)),
            "ln_beta": bf(0.1 * np.random.standard_normal(E))}


def reference(h_attn, x, out_w, ln_gamma, ln_beta):
    merged = f64(h_attn).transpose(0, 2, 1, 3).reshape(B, S, E)
    out = mxq(merged, 2, "e4m3") @ mxq(f64(out_w), 0, "e4m3")
    y = out + f64(x)
    mean = y.mean(-1, keepdims=True)
    var = np.square(y - mean).mean(-1, keepdims=True)
    return (y - mean) / np.sqrt(var + LN_EPS) * f64(ln_gamma) + f64(ln_beta)

@@ -1,0 +1,216 @@
+from contextlib import ExitStack
+
+import concourse.bass as bass
+import concourse.mybir as mybir
+import concourse.tile as tile
+from concourse.masks import make_identity
+
+FP8X4 = mybir.dt.float8_e4m3fn_x4
+BF16 = mybir.dt.bfloat16
+F32 = mybir.dt.float32
+U32 = mybir.dt.uint32
+U8 = mybir.dt.uint8
+ALU = mybir.AluOpType
+ACT = mybir.ActivationFunctionType
+
+B, H, S, D = 4, 4, 2048, 128
+E = H * D
+P = 128
+T = S // P
+CH = 4
+NCH = B * T // CH
+LN_EPS = 1e-6
+FLOPS = 2 * B * S * E * E
+
+G_TILES = 2
+Y_BUFS = 6
+
+
+def tile_selfattention_pa_t_kernel(tc, h_attn, x, out_w, ln_gamma, ln_beta, out):
+    nc = tc.nc
+    with ExitStack() as ctx:
+        const = ctx.enter_context(tc.tile_pool(name="const", bufs=1))
+        inp = ctx.enter_context(tc.tile_pool(name="inp", bufs=1))
+        ypool = ctx.enter_context(tc.tile_pool(name="ypool", bufs=Y_BUFS))
+        gpool = ctx.enter_context(tc.tile_pool(name="gpool", bufs=3))
+        small = ctx.enter_context(tc.tile_pool(name="small", bufs=Y_BUFS))
+        jpool = ctx.enter_context(tc.tile_pool(name="jpool", bufs=2))
+        ps_const = ctx.enter_context(tc.psum_pool(name="ps_const", bufs=1))
+        ps_t = ctx.enter_context(tc.psum_pool(name="ps_t", bufs=2))
+        ps_o = ctx.enter_context(tc.psum_pool(name="ps_o", bufs=4))
+
+        w_raw = const.tile([P, H, E], BF16)
+        nc.sync.dma_start(out=w_raw[:], in_=out_w.rearrange("(h p) n -> p h n", p=P))
+        gb_row = const.tile([P, 2 * E], BF16)
+        nc.vector.memset(gb_row[:], 0.0)
+
+        groups = [(0, 0, 4), (0, 4, 4), (0, 8, 4), (0, 12, 4), (1, 0, 16), (2, 0, 16), (3, 0, 16)]
+        where = {}
+        for gi, (b, t0, nt) in enumerate(groups):
+            hs = inp.tile([P, H, nt, D], BF16, name="h_%d_%d" % (b, t0))
+            nc.sync.dma_start(
+                out=hs[:],
+                in_=h_attn[b].rearrange("h (p t) d -> p h t d", t=T)[:, :, t0 : t0 + nt, :],
+            )
+            xs = inp.tile([P, nt, E], BF16, name="x_%d_%d" % (b, t0))
+            nc.sync.dma_start(
+                out=xs[:], in_=x[b].rearrange("(p t) n -> p t n", t=T)[:, t0 : t0 + nt, :]
+            )
+            for t in range(t0, t0 + nt):
+                where[(b, t)] = (hs, xs, t - t0)
+            if gi == 0:
+                nc.sync.dma_start(
+                    out=gb_row[0:1, 0:E], in_=ln_gamma.rearrange("(o n) -> o n", o=1)
+                )
+                nc.sync.dma_start(
+                    out=gb_row[0:1, E : 2 * E], in_=ln_beta.rearrange("(o n) -> o n", o=1)
+                )
+
+        ident = const.tile([P, P], BF16)
+        make_identity(nc, ident[:])
+        ones = const.tile([P, P], BF16)
+        nc.vector.memset(ones[:], 1.0)
+        eps = const.tile([P, 1], F32)
+        nc.vector.memset(eps[:], LN_EPS)
+
+        w_grp = const.tile([P, E, H], BF16, align_bytes=64)
+        nc.vector.tensor_copy(out=w_grp[:], in_=w_raw[:].rearrange("p h n -> p n h"))
+        w_codes = const.tile([P, E], U32, align_bytes=64)
+        w_scl = const.tile([P, E], U8, align_bytes=64)
+        nc.vector.quantize_mx(
+            out=w_codes[:].bitcast(FP8X4),
+            scales=w_scl[:],
+            in_=w_grp[:].rearrange("p n h -> p (n h)"),
+        )
+
+        g_ps = ps_const.tile([P, E], F32)
+        b_ps = ps_const.tile([P, E], F32)
+        nc.tensor.matmul(out=g_ps[:], lhsT=ones[:], rhs=gb_row[:, 0:E], start=True, stop=True)
+        nc.tensor.matmul(out=b_ps[:], lhsT=ones[:], rhs=gb_row[:, E : 2 * E], start=True, stop=True)
+        g_sb = const.tile([P, E], F32)
+        b_sb = const.tile([P, E], F32)
+        if G_TILES:
+            nc.vector.tensor_copy(out=g_sb[:], in_=g_ps[:])
+            nc.vector.tensor_copy(out=b_sb[:], in_=b_ps[:])
+
+        state = {}
+
+        def front(c):
+            b, t0 = divmod(c * CH, T)
+            grp = gpool.tile([P, CH, P, H], BF16, align_bytes=64, name="grp")
+            for half in range(CH // 2):
+                tp = ps_t.tile([P, 2, H, P], BF16, name="tp")
+                for j in range(2):
+                    hs, xs, tl = where[(b, t0 + 2 * half + j)]
+                    for h in range(H):
+                        nc.tensor.transpose(out=tp[:, j, h, :], in_=hs[:, h, tl, :], identity=ident[:])
+                nc.scalar.copy(
+                    out=grp[:, 2 * half : 2 * half + 2, :, :],
+                    in_=tp[:].rearrange("p i h s -> p i s h"),
+                )
+            codes = gpool.tile([P, CH * P], U32, align_bytes=64, name="codes")
+            scl = gpool.tile([P, CH * P], U8, align_bytes=64, name="scl")
+            nc.vector.quantize_mx(
+                out=codes[:].bitcast(FP8X4),
+                scales=scl[:],
+                in_=grp[:].rearrange("p i s h -> p (i s h)"),
+            )
+            y = ypool.tile([P, CH, E], F32, name="y")
+            sums = small.tile([P, CH], F32, name="sums")
+            for i in range(CH):
+                hs, xs, tl = where[(b, t0 + i)]
+                o_ps = ps_o.tile([P, E], F32, name="o_ps")
+                nc.tensor.matmul_mx(
+                    out=o_ps[:],
+                    lhsT=codes[:, i * P : (i + 1) * P].bitcast(FP8X4),
+                    lhsT_scale=scl[:, i * P : (i + 1) * P],
+                    rhs=w_codes[:].bitcast(FP8X4),
+                    rhs_scale=w_scl[:],
+                    start=True,
+                    stop=True,
+                )
+                nc.vector.scalar_tensor_tensor(
+                    out=y[:, i, :],
+                    in0=o_ps[:],
+                    scalar=0.0,
+                    in1=xs[:, tl, :],
+                    op0=ALU.add,
+                    op1=ALU.add,
+                    accum_out=sums[:, i : i + 1],
+                )
+            nm = small.tile([P, CH], F32, name="nm")
+            nc.vector.tensor_scalar(
+                out=nm[:], in0=sums[:], scalar1=-1.0 / E, scalar2=None, op0=ALU.mult
+            )
+            state[c] = (y, nm)
+
+        def back(c):
+            b, t0 = divmod(c * CH, T)
+            y, nm = state[c]
+            ssq = small.tile([P, CH], F32, name="ssq")
+            for i in range(CH):
+                junk = jpool.tile([P, E], BF16, name="junk")
+                nc.scalar.activation(
+                    out=junk[:],
+                    in_=y[:, i, :],
+                    func=ACT.Square,
+                    bias=nm[:, i : i + 1],
+                    scale=1.0,
+                    accum_out=ssq[:, i : i + 1],
+                )
+            std = small.tile([P, CH], F32, name="std")
+            nc.scalar.activation(
+                out=std[:], in_=ssq[:], func=ACT.Sqrt, bias=eps[:, 0:1], scale=1.0 / E
+            )
+            rstd = small.tile([P, CH], F32, name="rstd")
+            nc.vector.reciprocal(out=rstd[:], in_=std[:])
+            nv = CH - G_TILES
+            if G_TILES:
+                nmr = small.tile([P, CH], F32, name="nmr")
+                nc.vector.tensor_tensor(out=nmr[:], in0=nm[:], in1=rstd[:], op=ALU.mult)
+                for i in range(nv, CH):
+                    nc.scalar.activation(
+                        out=y[:, i, :],
+                        in_=y[:, i, :],
+                        func=ACT.Identity,
+                        bias=nmr[:, i : i + 1],
+                        scale=rstd[:, i : i + 1],
+                    )
+                nc.gpsimd.tensor_tensor(
+                    out=y[:, nv:CH, :],
+                    in0=y[:, nv:CH, :],
+                    in1=g_sb[:].unsqueeze(1).to_broadcast([P, G_TILES, E]),
+                    op=ALU.mult,
+                )
+                nc.gpsimd.tensor_tensor(
+                    out=y[:, nv:CH, :],
+                    in0=y[:, nv:CH, :],
+                    in1=b_sb[:].unsqueeze(1).to_broadcast([P, G_TILES, E]),
+                    op=ALU.add,
+                )
+            for i in range(nv):
+                nc.vector.scalar_tensor_tensor(
+                    out=y[:, i, :],
+                    in0=y[:, i, :],
+                    scalar=nm[:, i : i + 1],
+                    in1=g_ps[:],
+                    op0=ALU.add,
+                    op1=ALU.mult,
+                )
+                nc.vector.scalar_tensor_tensor(
+                    out=y[:, i, :],
+                    in0=y[:, i, :],
+                    scalar=rstd[:, i : i + 1],
+                    in1=b_ps[:],
+                    op0=ALU.mult,
+                    op1=ALU.add,
+                )
+            nc.sync.dma_start(
+                out=out[b].rearrange("(p t) n -> p t n", t=T)[:, t0 : t0 + CH, :], in_=y[:]
+            )
+
+        front(0)
+        for c in range(NCH):
+            if c + 1 < NCH:
+                front(c + 1)
+            back(c)

@@ -1,8 +1,6 @@
 from contextlib import ExitStack
 
-import concourse.bass as bass
 import concourse.mybir as mybir
-import concourse.tile as tile
 from concourse.masks import make_identity
 
 FP8X4 = mybir.dt.float8_e4m3fn_x4
@@ -22,13 +20,20 @@ NCH = B * T // CH
 LN_EPS = 1e-6
 FLOPS = 2 * B * S * E * E
 
-G_TILES = 2
+MANUAL = True
 Y_BUFS = 6
+G_SPLIT = 1
+
+
+def g_tiles(c):
+    return 0 if c == NCH - 1 else 2
 
 
 def tile_selfattention_pa_t_kernel(tc, h_attn, x, out_w, ln_gamma, ln_beta, out):
     nc = tc.nc
     with ExitStack() as ctx:
+        if MANUAL:
+            ctx.enter_context(tc.manual_schedule())
         const = ctx.enter_context(tc.tile_pool(name="const", bufs=1))
         inp = ctx.enter_context(tc.tile_pool(name="inp", bufs=1))
         ypool = ctx.enter_context(tc.tile_pool(name="ypool", bufs=Y_BUFS))
@@ -39,11 +44,18 @@ def tile_selfattention_pa_t_kernel(tc, h_attn, x, out_w, ln_gamma, ln_beta, out)
         ps_t = ctx.enter_context(tc.psum_pool(name="ps_t", bufs=2))
         ps_o = ctx.enter_context(tc.psum_pool(name="ps_o", bufs=4))
 
-        w_raw = const.tile([P, H, E], BF16)
-        nc.sync.dma_start(out=w_raw[:], in_=out_w.rearrange("(h p) n -> p h n", p=P))
+        ident = const.tile([P, P], BF16)
+        make_identity(nc, ident[:])
         gb_row = const.tile([P, 2 * E], BF16)
         nc.vector.memset(gb_row[:], 0.0)
+        ones = const.tile([P, P], BF16)
+        nc.vector.memset(ones[:], 1.0)
+        eps = const.tile([P, 1], F32)
+        nc.vector.memset(eps[:], LN_EPS)
+        warm = const.tile([P, 1], F32)
+        nc.scalar.activation(out=warm[:], in_=eps[:], func=ACT.Abs_reciprocal_sqrt)
 
+        w_raw = const.tile([P, H, E], BF16)
         groups = [(0, 0, 4), (0, 4, 4), (0, 8, 4), (0, 12, 4), (1, 0, 16), (2, 0, 16), (3, 0, 16)]
         where = {}
         for gi, (b, t0, nt) in enumerate(groups):
@@ -52,26 +64,20 @@ def tile_selfattention_pa_t_kernel(tc, h_attn, x, out_w, ln_gamma, ln_beta, out)
                 out=hs[:],
                 in_=h_attn[b].rearrange("h (p t) d -> p h t d", t=T)[:, :, t0 : t0 + nt, :],
             )
-            xs = inp.tile([P, nt, E], BF16, name="x_%d_%d" % (b, t0))
-            nc.sync.dma_start(
-                out=xs[:], in_=x[b].rearrange("(p t) n -> p t n", t=T)[:, t0 : t0 + nt, :]
-            )
-            for t in range(t0, t0 + nt):
-                where[(b, t)] = (hs, xs, t - t0)
             if gi == 0:
+                nc.sync.dma_start(out=w_raw[:], in_=out_w.rearrange("(h p) n -> p h n", p=P))
                 nc.sync.dma_start(
                     out=gb_row[0:1, 0:E], in_=ln_gamma.rearrange("(o n) -> o n", o=1)
                 )
                 nc.sync.dma_start(
                     out=gb_row[0:1, E : 2 * E], in_=ln_beta.rearrange("(o n) -> o n", o=1)
                 )
-
-        ident = const.tile([P, P], BF16)
-        make_identity(nc, ident[:])
-        ones = const.tile([P, P], BF16)
-        nc.vector.memset(ones[:], 1.0)
-        eps = const.tile([P, 1], F32)
-        nc.vector.memset(eps[:], LN_EPS)
+            xs = inp.tile([P, nt, E], BF16, name="x_%d_%d" % (b, t0))
+            nc.sync.dma_start(
+                out=xs[:], in_=x[b].rearrange("(p t) n -> p t n", t=T)[:, t0 : t0 + nt, :]
+            )
+            for t in range(t0, t0 + nt):
+                where[(b, t)] = (hs, xs, t - t0)
 
         w_grp = const.tile([P, E, H], BF16, align_bytes=64)
         nc.vector.tensor_copy(out=w_grp[:], in_=w_raw[:].rearrange("p h n -> p n h"))
@@ -83,42 +89,47 @@ def tile_selfattention_pa_t_kernel(tc, h_attn, x, out_w, ln_gamma, ln_beta, out)
             in_=w_grp[:].rearrange("p n h -> p (n h)"),
         )
 
-        g_ps = ps_const.tile([P, E], F32)
-        b_ps = ps_const.tile([P, E], F32)
-        nc.tensor.matmul(out=g_ps[:], lhsT=ones[:], rhs=gb_row[:, 0:E], start=True, stop=True)
-        nc.tensor.matmul(out=b_ps[:], lhsT=ones[:], rhs=gb_row[:, E : 2 * E], start=True, stop=True)
-        g_sb = const.tile([P, E], F32)
-        b_sb = const.tile([P, E], F32)
-        if G_TILES:
-            nc.vector.tensor_copy(out=g_sb[:], in_=g_ps[:])
-            nc.vector.tensor_copy(out=b_sb[:], in_=b_ps[:])
+        st = {}
 
-        state = {}
+        def rows(c):
+            return divmod(c * CH, T)
 
-        def front(c):
-            b, t0 = divmod(c * CH, T)
-            grp = gpool.tile([P, CH, P, H], BF16, align_bytes=64, name="grp")
+        def transposes(c):
+            b, t0 = rows(c)
+            tps = []
             for half in range(CH // 2):
                 tp = ps_t.tile([P, 2, H, P], BF16, name="tp")
                 for j in range(2):
                     hs, xs, tl = where[(b, t0 + 2 * half + j)]
                     for h in range(H):
                         nc.tensor.transpose(out=tp[:, j, h, :], in_=hs[:, h, tl, :], identity=ident[:])
+                tps.append(tp)
+            st[c] = {"tp": tps}
+
+        def regroup(c):
+            grp = gpool.tile([P, CH, P, H], BF16, align_bytes=64, name="grp")
+            for half in range(CH // 2):
                 nc.scalar.copy(
                     out=grp[:, 2 * half : 2 * half + 2, :, :],
-                    in_=tp[:].rearrange("p i h s -> p i s h"),
+                    in_=st[c]["tp"][half][:].rearrange("p i h s -> p i s h"),
                 )
+            st[c]["grp"] = grp
+
+        def quantise(c):
             codes = gpool.tile([P, CH * P], U32, align_bytes=64, name="codes")
             scl = gpool.tile([P, CH * P], U8, align_bytes=64, name="scl")
             nc.vector.quantize_mx(
                 out=codes[:].bitcast(FP8X4),
                 scales=scl[:],
-                in_=grp[:].rearrange("p i s h -> p (i s h)"),
+                in_=st[c]["grp"][:].rearrange("p i s h -> p (i s h)"),
             )
-            y = ypool.tile([P, CH, E], F32, name="y")
-            sums = small.tile([P, CH], F32, name="sums")
+            st[c]["codes"] = codes
+            st[c]["scl"] = scl
+
+        def project(c):
+            codes, scl = st[c]["codes"], st[c]["scl"]
+            banks = []
             for i in range(CH):
-                hs, xs, tl = where[(b, t0 + i)]
                 o_ps = ps_o.tile([P, E], F32, name="o_ps")
                 nc.tensor.matmul_mx(
                     out=o_ps[:],
@@ -129,24 +140,31 @@ def tile_selfattention_pa_t_kernel(tc, h_attn, x, out_w, ln_gamma, ln_beta, out)
                     start=True,
                     stop=True,
                 )
+                banks.append(o_ps)
+            st[c]["o"] = banks
+
+        def residual(c):
+            b, t0 = rows(c)
+            y = ypool.tile([P, CH, E], F32, name="y")
+            sums = small.tile([P, CH], F32, name="sums")
+            for i in range(CH):
+                hs, xs, tl = where[(b, t0 + i)]
                 nc.vector.scalar_tensor_tensor(
                     out=y[:, i, :],
-                    in0=o_ps[:],
+                    in0=st[c]["o"][i][:],
                     scalar=0.0,
                     in1=xs[:, tl, :],
                     op0=ALU.add,
                     op1=ALU.add,
                     accum_out=sums[:, i : i + 1],
                 )
-            nm = small.tile([P, CH], F32, name="nm")
-            nc.vector.tensor_scalar(
-                out=nm[:], in0=sums[:], scalar1=-1.0 / E, scalar2=None, op0=ALU.mult
-            )
-            state[c] = (y, nm)
+            st[c]["y"] = y
+            st[c]["sums"] = sums
 
-        def back(c):
-            b, t0 = divmod(c * CH, T)
-            y, nm = state[c]
+        def squares(c):
+            y = st[c]["y"]
+            nm = small.tile([P, CH], F32, name="nm")
+            nc.scalar.activation(out=nm[:], in_=st[c]["sums"][:], func=ACT.Copy, scale=-1.0 / E)
             ssq = small.tile([P, CH], F32, name="ssq")
             for i in range(CH):
                 junk = jpool.tile([P, E], BF16, name="junk")
@@ -158,37 +176,12 @@ def tile_selfattention_pa_t_kernel(tc, h_attn, x, out_w, ln_gamma, ln_beta, out)
                     scale=1.0,
                     accum_out=ssq[:, i : i + 1],
                 )
-            std = small.tile([P, CH], F32, name="std")
-            nc.scalar.activation(
-                out=std[:], in_=ssq[:], func=ACT.Sqrt, bias=eps[:, 0:1], scale=1.0 / E
-            )
-            rstd = small.tile([P, CH], F32, name="rstd")
-            nc.vector.reciprocal(out=rstd[:], in_=std[:])
-            nv = CH - G_TILES
-            if G_TILES:
-                nmr = small.tile([P, CH], F32, name="nmr")
-                nc.vector.tensor_tensor(out=nmr[:], in0=nm[:], in1=rstd[:], op=ALU.mult)
-                for i in range(nv, CH):
-                    nc.scalar.activation(
-                        out=y[:, i, :],
-                        in_=y[:, i, :],
-                        func=ACT.Identity,
-                        bias=nmr[:, i : i + 1],
-                        scale=rstd[:, i : i + 1],
-                    )
-                nc.gpsimd.tensor_tensor(
-                    out=y[:, nv:CH, :],
-                    in0=y[:, nv:CH, :],
-                    in1=g_sb[:].unsqueeze(1).to_broadcast([P, G_TILES, E]),
-                    op=ALU.mult,
-                )
-                nc.gpsimd.tensor_tensor(
-                    out=y[:, nv:CH, :],
-                    in0=y[:, nv:CH, :],
-                    in1=b_sb[:].unsqueeze(1).to_broadcast([P, G_TILES, E]),
-                    op=ALU.add,
-                )
-            for i in range(nv):
+            st[c]["nm"] = nm
+            st[c]["ssq"] = ssq
+
+        def centre_gamma(c):
+            y, nm = st[c]["y"], st[c]["nm"]
+            for i in range(CH - g_tiles(c)):
                 nc.vector.scalar_tensor_tensor(
                     out=y[:, i, :],
                     in0=y[:, i, :],
@@ -197,6 +190,39 @@ def tile_selfattention_pa_t_kernel(tc, h_attn, x, out_w, ln_gamma, ln_beta, out)
                     op0=ALU.add,
                     op1=ALU.mult,
                 )
+
+        def rstd_normalise(c):
+            y, nm = st[c]["y"], st[c]["nm"]
+            rstd = small.tile([P, CH], F32, name="rstd")
+            nc.scalar.activation(
+                out=rstd[:],
+                in_=st[c]["ssq"][:],
+                func=ACT.Abs_reciprocal_sqrt,
+                bias=eps[:, 0:1],
+                scale=1.0 / E,
+            )
+            st[c]["rstd"] = rstd
+            if g_tiles(c):
+                nmr = small.tile([P, CH], F32, name="nmr")
+                for i in range(CH - g_tiles(c), CH):
+                    nc.scalar.activation(
+                        out=nmr[:, i : i + 1],
+                        in_=nm[:, i : i + 1],
+                        func=ACT.Copy,
+                        scale=rstd[:, i : i + 1],
+                    )
+                for i in range(CH - g_tiles(c), CH):
+                    nc.scalar.activation(
+                        out=y[:, i, :],
+                        in_=y[:, i, :],
+                        func=ACT.Identity,
+                        bias=nmr[:, i : i + 1],
+                        scale=rstd[:, i : i + 1],
+                    )
+
+        def scale_beta(c):
+            y, rstd = st[c]["y"], st[c]["rstd"]
+            for i in range(CH - g_tiles(c)):
                 nc.vector.scalar_tensor_tensor(
                     out=y[:, i, :],
                     in0=y[:, i, :],
@@ -205,12 +231,61 @@ def tile_selfattention_pa_t_kernel(tc, h_attn, x, out_w, ln_gamma, ln_beta, out)
                     op0=ALU.mult,
                     op1=ALU.add,
                 )
-            nc.sync.dma_start(
-                out=out[b].rearrange("(p t) n -> p t n", t=T)[:, t0 : t0 + CH, :], in_=y[:]
-            )
 
-        front(0)
-        for c in range(NCH):
-            if c + 1 < NCH:
-                front(c + 1)
-            back(c)
+        def gpsimd_affine(c):
+            y = st[c]["y"]
+            n = g_tiles(c)
+            if n:
+                step = n // G_SPLIT
+                for vec, op in ((g_sb, ALU.mult), (b_sb, ALU.add)):
+                    for lo in range(CH - n, CH, step):
+                        nc.gpsimd.tensor_tensor(
+                            out=y[:, lo : lo + step, :],
+                            in0=y[:, lo : lo + step, :],
+                            in1=vec[:].unsqueeze(1).to_broadcast([P, step, E]),
+                            op=op,
+                        )
+
+        def store(c):
+            b, t0 = rows(c)
+            dst = out[b].rearrange("(p t) n -> p t n", t=T)
+            parts = 2 if c == NCH - 1 else 1
+            w = CH // parts
+            for q in range(parts):
+                nc.sync.dma_start(
+                    out=dst[:, t0 + q * w : t0 + (q + 1) * w, :],
+                    in_=st[c]["y"][:, q * w : (q + 1) * w, :],
+                )
+
+        transposes(0)
+        regroup(0)
+
+        g_ps = ps_const.tile([P, E], F32)
+        b_ps = ps_const.tile([P, E], F32)
+        nc.tensor.matmul(out=g_ps[:], lhsT=ones[:], rhs=gb_row[:, 0:E], start=True, stop=True)
+        nc.tensor.matmul(out=b_ps[:], lhsT=ones[:], rhs=gb_row[:, E : 2 * E], start=True, stop=True)
+        g_sb = const.tile([P, E], F32)
+        b_sb = const.tile([P, E], F32)
+
+        for k in range(NCH + 2):
+            if k + 1 < NCH:
+                transposes(k + 1)
+            if k >= 2:
+                scale_beta(k - 2)
+                gpsimd_affine(k - 2)
+                store(k - 2)
+            if k < NCH:
+                quantise(k)
+                project(k)
+            if k == 0:
+                nc.vector.tensor_copy(out=g_sb[:], in_=g_ps[:])
+                nc.vector.tensor_copy(out=b_sb[:], in_=b_ps[:])
+            if 1 <= k <= NCH:
+                squares(k - 1)
+                centre_gamma(k - 1)
+            if k < NCH:
+                residual(k)
+            if k + 1 < NCH:
+                regroup(k + 1)
+            if 1 <= k <= NCH:
+                rstd_normalise(k - 1)

@@ -20,7 +20,7 @@ NCH = B * T // CH
 LN_EPS = 1e-6
 FLOPS = 2 * B * S * E * E
 
-MANUAL = True
+MANUAL = False
 Y_BUFS = 6
 G_SPLIT = 1
 

@@ -15,22 +15,30 @@ B, H, S, D = 4, 4, 2048, 128
 E = H * D
 P = 128
 T = S // P
-CH = 4
-NCH = B * T // CH
 LN_EPS = 1e-6
 FLOPS = 2 * B * S * E * E
 
-MANUAL = False
+MANUAL = True
 Y_BUFS = 6
-G_SPLIT = 1
+SIZES = [4] * 15 + [2, 2]
+LOADS = [(0, 0, 4), (0, 4, 4), (0, 8, 4), (0, 12, 4), (1, 0, 16), (2, 0, 16), (3, 0, 16)]
+NCH = len(SIZES)
+G_LAST = 13
+G_FIRST = 0
+G_STEP = 1
 
 
 def g_tiles(c):
-    return 0 if c == NCH - 1 else 2
+    return 2 if G_FIRST <= c <= G_LAST else 0
+
+
+def g_norm(c):
+    return 0
 
 
 def tile_selfattention_pa_t_kernel(tc, h_attn, x, out_w, ln_gamma, ln_beta, out):
     nc = tc.nc
+    starts = [sum(SIZES[:c]) for c in range(NCH)]
     with ExitStack() as ctx:
         if MANUAL:
             ctx.enter_context(tc.manual_schedule())
@@ -38,7 +46,7 @@ def tile_selfattention_pa_t_kernel(tc, h_attn, x, out_w, ln_gamma, ln_beta, out)
         inp = ctx.enter_context(tc.tile_pool(name="inp", bufs=1))
         ypool = ctx.enter_context(tc.tile_pool(name="ypool", bufs=Y_BUFS))
         gpool = ctx.enter_context(tc.tile_pool(name="gpool", bufs=3))
-        small = ctx.enter_context(tc.tile_pool(name="small", bufs=Y_BUFS))
+        small = ctx.enter_context(tc.tile_pool(name="small", bufs=Y_BUFS + 1))
         jpool = ctx.enter_context(tc.tile_pool(name="jpool", bufs=2))
         ps_const = ctx.enter_context(tc.psum_pool(name="ps_const", bufs=1))
         ps_t = ctx.enter_context(tc.psum_pool(name="ps_t", bufs=2))
@@ -56,9 +64,8 @@ def tile_selfattention_pa_t_kernel(tc, h_attn, x, out_w, ln_gamma, ln_beta, out)
         nc.scalar.activation(out=warm[:], in_=eps[:], func=ACT.Abs_reciprocal_sqrt)
 
         w_raw = const.tile([P, H, E], BF16)
-        groups = [(0, 0, 4), (0, 4, 4), (0, 8, 4), (0, 12, 4), (1, 0, 16), (2, 0, 16), (3, 0, 16)]
         where = {}
-        for gi, (b, t0, nt) in enumerate(groups):
+        for gi, (b, t0, nt) in enumerate(LOADS):
             hs = inp.tile([P, H, nt, D], BF16, name="h_%d_%d" % (b, t0))
             nc.sync.dma_start(
                 out=hs[:],
@@ -66,62 +73,58 @@ def tile_selfattention_pa_t_kernel(tc, h_attn, x, out_w, ln_gamma, ln_beta, out)
             )
             if gi == 0:
                 nc.sync.dma_start(out=w_raw[:], in_=out_w.rearrange("(h p) n -> p h n", p=P))
+            xs = inp.tile([P, nt, E], BF16, name="x_%d_%d" % (b, t0))
+            nc.sync.dma_start(
+                out=xs[:], in_=x[b].rearrange("(p t) n -> p t n", t=T)[:, t0 : t0 + nt, :]
+            )
+            if gi == 0:
                 nc.sync.dma_start(
                     out=gb_row[0:1, 0:E], in_=ln_gamma.rearrange("(o n) -> o n", o=1)
                 )
                 nc.sync.dma_start(
                     out=gb_row[0:1, E : 2 * E], in_=ln_beta.rearrange("(o n) -> o n", o=1)
                 )
-            xs = inp.tile([P, nt, E], BF16, name="x_%d_%d" % (b, t0))
-            nc.sync.dma_start(
-                out=xs[:], in_=x[b].rearrange("(p t) n -> p t n", t=T)[:, t0 : t0 + nt, :]
-            )
             for t in range(t0, t0 + nt):
                 where[(b, t)] = (hs, xs, t - t0)
-
-        w_grp = const.tile([P, E, H], BF16, align_bytes=64)
-        nc.vector.tensor_copy(out=w_grp[:], in_=w_raw[:].rearrange("p h n -> p n h"))
-        w_codes = const.tile([P, E], U32, align_bytes=64)
-        w_scl = const.tile([P, E], U8, align_bytes=64)
-        nc.vector.quantize_mx(
-            out=w_codes[:].bitcast(FP8X4),
-            scales=w_scl[:],
-            in_=w_grp[:].rearrange("p n h -> p (n h)"),
-        )
 
         st = {}
 
         def rows(c):
-            return divmod(c * CH, T)
+            return divmod(starts[c], T)
 
         def transposes(c):
             b, t0 = rows(c)
             tps = []
-            for half in range(CH // 2):
+            for lo in range(0, SIZES[c], 2):
                 tp = ps_t.tile([P, 2, H, P], BF16, name="tp")
-                for j in range(2):
-                    hs, xs, tl = where[(b, t0 + 2 * half + j)]
+                for j in range(min(2, SIZES[c] - lo)):
+                    hs, xs, tl = where[(b, t0 + lo + j)]
                     for h in range(H):
                         nc.tensor.transpose(out=tp[:, j, h, :], in_=hs[:, h, tl, :], identity=ident[:])
                 tps.append(tp)
             st[c] = {"tp": tps}
 
-        def regroup(c):
-            grp = gpool.tile([P, CH, P, H], BF16, align_bytes=64, name="grp")
-            for half in range(CH // 2):
+        def regroup(c, q):
+            n = SIZES[c]
+            if q == 0:
+                grp = gpool.tile([P, 4, P, H], BF16, align_bytes=64, name="grp")
+                st[c]["grp"] = grp
+            lo = 2 * q
+            if lo < n:
+                w = min(2, n - lo)
                 nc.scalar.copy(
-                    out=grp[:, 2 * half : 2 * half + 2, :, :],
-                    in_=st[c]["tp"][half][:].rearrange("p i h s -> p i s h"),
+                    out=st[c]["grp"][:, lo : lo + w, :, :],
+                    in_=st[c]["tp"][q][:, 0:w, :, :].rearrange("p i h s -> p i s h"),
                 )
-            st[c]["grp"] = grp
 
         def quantise(c):
-            codes = gpool.tile([P, CH * P], U32, align_bytes=64, name="codes")
-            scl = gpool.tile([P, CH * P], U8, align_bytes=64, name="scl")
+            n = SIZES[c]
+            codes = gpool.tile([P, 4 * P], U32, align_bytes=64, name="codes")
+            scl = gpool.tile([P, 4 * P], U8, align_bytes=64, name="scl")
             nc.vector.quantize_mx(
-                out=codes[:].bitcast(FP8X4),
-                scales=scl[:],
-                in_=st[c]["grp"][:].rearrange("p i s h -> p (i s h)"),
+                out=codes[:, 0 : n * P].bitcast(FP8X4),
+                scales=scl[:, 0 : n * P],
+                in_=st[c]["grp"][:, 0:n, :, :].rearrange("p i s h -> p (i s h)"),
             )
             st[c]["codes"] = codes
             st[c]["scl"] = scl
@@ -129,7 +132,7 @@ def tile_selfattention_pa_t_kernel(tc, h_attn, x, out_w, ln_gamma, ln_beta, out)
         def project(c):
             codes, scl = st[c]["codes"], st[c]["scl"]
             banks = []
-            for i in range(CH):
+            for i in range(SIZES[c]):
                 o_ps = ps_o.tile([P, E], F32, name="o_ps")
                 nc.tensor.matmul_mx(
                     out=o_ps[:],
@@ -145,9 +148,9 @@ def tile_selfattention_pa_t_kernel(tc, h_attn, x, out_w, ln_gamma, ln_beta, out)
 
         def residual(c):
             b, t0 = rows(c)
-            y = ypool.tile([P, CH, E], F32, name="y")
-            sums = small.tile([P, CH], F32, name="sums")
-            for i in range(CH):
+            y = ypool.tile([P, 4, E], F32, name="y")
+            sums = small.tile([P, 4], F32, name="sums")
+            for i in range(SIZES[c]):
                 hs, xs, tl = where[(b, t0 + i)]
                 nc.vector.scalar_tensor_tensor(
                     out=y[:, i, :],
@@ -161,12 +164,18 @@ def tile_selfattention_pa_t_kernel(tc, h_attn, x, out_w, ln_gamma, ln_beta, out)
             st[c]["y"] = y
             st[c]["sums"] = sums
 
+        def neg_mean(c):
+            n = SIZES[c]
+            nm = small.tile([P, 4], F32, name="nm")
+            nc.scalar.activation(
+                out=nm[:, 0:n], in_=st[c]["sums"][:, 0:n], func=ACT.Copy, scale=-1.0 / E
+            )
+            st[c]["nm"] = nm
+
         def squares(c):
-            y = st[c]["y"]
-            nm = small.tile([P, CH], F32, name="nm")
-            nc.scalar.activation(out=nm[:], in_=st[c]["sums"][:], func=ACT.Copy, scale=-1.0 / E)
-            ssq = small.tile([P, CH], F32, name="ssq")
-            for i in range(CH):
+            y, nm = st[c]["y"], st[c]["nm"]
+            ssq = small.tile([P, 4], F32, name="ssq")
+            for i in range(SIZES[c]):
                 junk = jpool.tile([P, E], BF16, name="junk")
                 nc.scalar.activation(
                     out=junk[:],
@@ -176,12 +185,11 @@ def tile_selfattention_pa_t_kernel(tc, h_attn, x, out_w, ln_gamma, ln_beta, out)
                     scale=1.0,
                     accum_out=ssq[:, i : i + 1],
                 )
-            st[c]["nm"] = nm
             st[c]["ssq"] = ssq
 
         def centre_gamma(c):
             y, nm = st[c]["y"], st[c]["nm"]
-            for i in range(CH - g_tiles(c)):
+            for i in range(SIZES[c] - g_tiles(c)):
                 nc.vector.scalar_tensor_tensor(
                     out=y[:, i, :],
                     in0=y[:, i, :],
@@ -191,38 +199,49 @@ def tile_selfattention_pa_t_kernel(tc, h_attn, x, out_w, ln_gamma, ln_beta, out)
                     op1=ALU.mult,
                 )
 
-        def rstd_normalise(c):
-            y, nm = st[c]["y"], st[c]["nm"]
-            rstd = small.tile([P, CH], F32, name="rstd")
+        def inv_std(c):
+            n = SIZES[c]
+            rstd = small.tile([P, 4], F32, name="rstd")
             nc.scalar.activation(
-                out=rstd[:],
-                in_=st[c]["ssq"][:],
+                out=rstd[:, 0:n],
+                in_=st[c]["ssq"][:, 0:n],
                 func=ACT.Abs_reciprocal_sqrt,
                 bias=eps[:, 0:1],
                 scale=1.0 / E,
             )
             st[c]["rstd"] = rstd
-            if g_tiles(c):
-                nmr = small.tile([P, CH], F32, name="nmr")
-                for i in range(CH - g_tiles(c), CH):
+
+        def on_scalar(c):
+            return list(range(SIZES[c] - g_tiles(c), SIZES[c] - g_norm(c))) if g_tiles(c) else []
+
+        def shifts(c):
+            nm, rstd = st[c]["nm"], st[c]["rstd"]
+            if on_scalar(c):
+                nmr = small.tile([P, 4], F32, name="nmr")
+                st[c]["nmr"] = nmr
+                for i in on_scalar(c):
                     nc.scalar.activation(
                         out=nmr[:, i : i + 1],
                         in_=nm[:, i : i + 1],
                         func=ACT.Copy,
                         scale=rstd[:, i : i + 1],
                     )
-                for i in range(CH - g_tiles(c), CH):
-                    nc.scalar.activation(
-                        out=y[:, i, :],
-                        in_=y[:, i, :],
-                        func=ACT.Identity,
-                        bias=nmr[:, i : i + 1],
-                        scale=rstd[:, i : i + 1],
-                    )
+
+        def normalise(c, j):
+            if j < len(on_scalar(c)):
+                i = on_scalar(c)[j]
+                y = st[c]["y"]
+                nc.scalar.activation(
+                    out=y[:, i, :],
+                    in_=y[:, i, :],
+                    func=ACT.Identity,
+                    bias=st[c]["nmr"][:, i : i + 1],
+                    scale=st[c]["rstd"][:, i : i + 1],
+                )
 
         def scale_beta(c):
             y, rstd = st[c]["y"], st[c]["rstd"]
-            for i in range(CH - g_tiles(c)):
+            for i in range(SIZES[c] - g_tiles(c)):
                 nc.vector.scalar_tensor_tensor(
                     out=y[:, i, :],
                     in0=y[:, i, :],
@@ -233,59 +252,95 @@ def tile_selfattention_pa_t_kernel(tc, h_attn, x, out_w, ln_gamma, ln_beta, out)
                 )
 
         def gpsimd_affine(c):
-            y = st[c]["y"]
-            n = g_tiles(c)
-            if n:
-                step = n // G_SPLIT
+            y, nm, rstd = st[c]["y"], st[c]["nm"], st[c]["rstd"]
+            n = SIZES[c]
+            g = g_tiles(c)
+            if g:
+                for i in range(n - g_norm(c), n):
+                    nc.gpsimd.tensor_scalar(
+                        out=y[:, i, :],
+                        in0=y[:, i, :],
+                        scalar1=nm[:, i : i + 1],
+                        scalar2=rstd[:, i : i + 1],
+                        op0=ALU.add,
+                        op1=ALU.mult,
+                    )
                 for vec, op in ((g_sb, ALU.mult), (b_sb, ALU.add)):
-                    for lo in range(CH - n, CH, step):
+                    for i in range(n - g, n, G_STEP):
                         nc.gpsimd.tensor_tensor(
-                            out=y[:, lo : lo + step, :],
-                            in0=y[:, lo : lo + step, :],
-                            in1=vec[:].unsqueeze(1).to_broadcast([P, step, E]),
+                            out=y[:, i : i + G_STEP, :],
+                            in0=y[:, i : i + G_STEP, :],
+                            in1=vec[:].unsqueeze(1).to_broadcast([P, G_STEP, E]),
                             op=op,
                         )
 
         def store(c):
             b, t0 = rows(c)
-            dst = out[b].rearrange("(p t) n -> p t n", t=T)
-            parts = 2 if c == NCH - 1 else 1
-            w = CH // parts
-            for q in range(parts):
-                nc.sync.dma_start(
-                    out=dst[:, t0 + q * w : t0 + (q + 1) * w, :],
-                    in_=st[c]["y"][:, q * w : (q + 1) * w, :],
-                )
+            n = SIZES[c]
+            nc.sync.dma_start(
+                out=out[b].rearrange("(p t) n -> p t n", t=T)[:, t0 : t0 + n, :],
+                in_=st[c]["y"][:, 0:n, :],
+            )
 
         transposes(0)
-        regroup(0)
+        regroup(0, 0)
+        regroup(0, 1)
+
+        w_grp = const.tile([P, E, H], BF16, align_bytes=64)
+        nc.vector.tensor_copy(out=w_grp[:], in_=w_raw[:].rearrange("p h n -> p n h"))
+        w_codes = const.tile([P, E], U32, align_bytes=64)
+        w_scl = const.tile([P, E], U8, align_bytes=64)
+        nc.vector.quantize_mx(
+            out=w_codes[:].bitcast(FP8X4),
+            scales=w_scl[:],
+            in_=w_grp[:].rearrange("p n h -> p (n h)"),
+        )
 
         g_ps = ps_const.tile([P, E], F32)
         b_ps = ps_const.tile([P, E], F32)
-        nc.tensor.matmul(out=g_ps[:], lhsT=ones[:], rhs=gb_row[:, 0:E], start=True, stop=True)
-        nc.tensor.matmul(out=b_ps[:], lhsT=ones[:], rhs=gb_row[:, E : 2 * E], start=True, stop=True)
         g_sb = const.tile([P, E], F32)
         b_sb = const.tile([P, E], F32)
 
-        for k in range(NCH + 2):
-            if k + 1 < NCH:
+        def live(c):
+            return 0 <= c < NCH
+
+        for k in range(NCH + 3):
+            if live(k + 1):
                 transposes(k + 1)
-            if k >= 2:
-                scale_beta(k - 2)
-                gpsimd_affine(k - 2)
-                store(k - 2)
-            if k < NCH:
+            if live(k):
                 quantise(k)
                 project(k)
             if k == 0:
-                nc.vector.tensor_copy(out=g_sb[:], in_=g_ps[:])
-                nc.vector.tensor_copy(out=b_sb[:], in_=b_ps[:])
-            if 1 <= k <= NCH:
+                nc.tensor.matmul(out=g_ps[:], lhsT=ones[:], rhs=gb_row[:, 0:E], start=True, stop=True)
+                nc.tensor.matmul(
+                    out=b_ps[:], lhsT=ones[:], rhs=gb_row[:, E : 2 * E], start=True, stop=True
+                )
+            if live(k - 2):
+                scale_beta(k - 2)
+                if not g_tiles(k - 2):
+                    store(k - 2)
+            if live(k - 3) and g_tiles(k - 3):
+                gpsimd_affine(k - 3)
+                store(k - 3)
+            if live(k):
+                residual(k)
+            if live(k - 1):
+                neg_mean(k - 1)
+            if live(k + 1):
+                regroup(k + 1, 0)
+            if live(k - 1):
                 squares(k - 1)
                 centre_gamma(k - 1)
-            if k < NCH:
-                residual(k)
-            if k + 1 < NCH:
-                regroup(k + 1)
-            if 1 <= k <= NCH:
-                rstd_normalise(k - 1)
+            if k == 1:
+                nc.vector.tensor_copy(out=g_sb[:], in_=g_ps[:])
+                nc.vector.tensor_copy(out=b_sb[:], in_=b_ps[:])
+            if live(k + 1):
+                regroup(k + 1, 1)
+            if live(k - 1):
+                inv_std(k - 1)
+            if live(k - 2):
+                normalise(k - 2, 0)
+            if live(k - 1):
+                shifts(k - 1)
+            if live(k - 2):
+                normalise(k - 2, 1)

@@ -14,14 +14,14 @@ ACT = mybir.ActivationFunctionType
 B, H, S, D = 4, 4, 2048, 128
 E = H * D
 P = 128
-T = S // P
+T = B * S // P
 LN_EPS = 1e-6
 FLOPS = 2 * B * S * E * E
 
 MANUAL = True
 Y_BUFS = 6
 SIZES = [4] * 15 + [2, 2]
-LOADS = [(0, 0, 4), (0, 4, 4), (0, 8, 4), (0, 12, 4), (1, 0, 16), (2, 0, 16), (3, 0, 16)]
+LOADS = [(0, 4), (4, 4), (8, 8), (16, 16), (32, 32)]
 NCH = len(SIZES)
 G_LAST = 13
 G_FIRST = 0
@@ -60,23 +60,26 @@ def tile_selfattention_pa_t_kernel(tc, h_attn, x, out_w, ln_gamma, ln_beta, out)
         nc.vector.memset(ones[:], 1.0)
         eps = const.tile([P, 1], F32)
         nc.vector.memset(eps[:], LN_EPS)
+        perm = const.tile([P, P], BF16)
+        nc.vector.tensor_copy(
+            out=perm[:].rearrange("p (q h) -> p q h", h=H),
+            in_=ident[:].rearrange("p (h q) -> p q h", h=H),
+        )
         warm = const.tile([P, 1], F32)
         nc.scalar.activation(out=warm[:], in_=eps[:], func=ACT.Abs_reciprocal_sqrt)
 
         w_raw = const.tile([P, H, E], BF16)
         where = {}
-        for gi, (b, t0, nt) in enumerate(LOADS):
-            hs = inp.tile([P, H, nt, D], BF16, name="h_%d_%d" % (b, t0))
-            nc.sync.dma_start(
-                out=hs[:],
-                in_=h_attn[b].rearrange("h (p t) d -> p h t d", t=T)[:, :, t0 : t0 + nt, :],
-            )
+        h_view = h_attn.rearrange("b h (q t) d -> (h q) b t d", t=T)
+        x_view = x.rearrange("b s n -> (b s) n").rearrange("(m t) n -> m t n", t=T)
+        out_view = out.rearrange("b s n -> (b s) n").rearrange("(m t) n -> m t n", t=T)
+        for gi, (t0, nt) in enumerate(LOADS):
+            hs = inp.tile([P, B, nt, D], BF16, name="h_%d" % t0)
+            nc.sync.dma_start(out=hs[:], in_=h_view[:, :, t0 : t0 + nt, :])
             if gi == 0:
                 nc.sync.dma_start(out=w_raw[:], in_=out_w.rearrange("(h p) n -> p h n", p=P))
-            xs = inp.tile([P, nt, E], BF16, name="x_%d_%d" % (b, t0))
-            nc.sync.dma_start(
-                out=xs[:], in_=x[b].rearrange("(p t) n -> p t n", t=T)[:, t0 : t0 + nt, :]
-            )
+            xs = inp.tile([P, nt, E], BF16, name="x_%d" % t0)
+            nc.sync.dma_start(out=xs[:], in_=x_view[:, t0 : t0 + nt, :])
             if gi == 0:
                 nc.sync.dma_start(
                     out=gb_row[0:1, 0:E], in_=ln_gamma.rearrange("(o n) -> o n", o=1)
@@ -85,36 +88,32 @@ def tile_selfattention_pa_t_kernel(tc, h_attn, x, out_w, ln_gamma, ln_beta, out)
                     out=gb_row[0:1, E : 2 * E], in_=ln_beta.rearrange("(o n) -> o n", o=1)
                 )
             for t in range(t0, t0 + nt):
-                where[(b, t)] = (hs, xs, t - t0)
+                where[t] = (hs, xs, t - t0)
 
         st = {}
 
-        def rows(c):
-            return divmod(starts[c], T)
-
         def transposes(c):
-            b, t0 = rows(c)
             tps = []
             for lo in range(0, SIZES[c], 2):
-                tp = ps_t.tile([P, 2, H, P], BF16, name="tp")
+                tp = ps_t.tile([P, 2, B, P], BF16, name="tp")
                 for j in range(min(2, SIZES[c] - lo)):
-                    hs, xs, tl = where[(b, t0 + lo + j)]
-                    for h in range(H):
-                        nc.tensor.transpose(out=tp[:, j, h, :], in_=hs[:, h, tl, :], identity=ident[:])
+                    hs, xs, tl = where[starts[c] + lo + j]
+                    for b in range(B):
+                        nc.tensor.transpose(out=tp[:, j, b, :], in_=hs[:, b, tl, :], identity=perm[:])
                 tps.append(tp)
             st[c] = {"tp": tps}
 
         def regroup(c, q):
             n = SIZES[c]
             if q == 0:
-                grp = gpool.tile([P, 4, P, H], BF16, align_bytes=64, name="grp")
+                grp = gpool.tile([P, 4, P * H], BF16, align_bytes=64, name="grp")
                 st[c]["grp"] = grp
             lo = 2 * q
             if lo < n:
                 w = min(2, n - lo)
                 nc.scalar.copy(
-                    out=st[c]["grp"][:, lo : lo + w, :, :],
-                    in_=st[c]["tp"][q][:, 0:w, :, :].rearrange("p i h s -> p i s h"),
+                    out=st[c]["grp"][:, lo : lo + w, :],
+                    in_=st[c]["tp"][q][:, 0:w, :, :].rearrange("p i b c -> p i (b c)"),
                 )
 
         def quantise(c):
@@ -124,7 +123,7 @@ def tile_selfattention_pa_t_kernel(tc, h_attn, x, out_w, ln_gamma, ln_beta, out)
             nc.vector.quantize_mx(
                 out=codes[:, 0 : n * P].bitcast(FP8X4),
                 scales=scl[:, 0 : n * P],
-                in_=st[c]["grp"][:, 0:n, :, :].rearrange("p i s h -> p (i s h)"),
+                in_=st[c]["grp"][:, 0:n, :].rearrange("p i c -> p (i c)"),
             )
             st[c]["codes"] = codes
             st[c]["scl"] = scl
@@ -147,11 +146,10 @@ def tile_selfattention_pa_t_kernel(tc, h_attn, x, out_w, ln_gamma, ln_beta, out)
             st[c]["o"] = banks
 
         def residual(c):
-            b, t0 = rows(c)
             y = ypool.tile([P, 4, E], F32, name="y")
             sums = small.tile([P, 4], F32, name="sums")
             for i in range(SIZES[c]):
-                hs, xs, tl = where[(b, t0 + i)]
+                hs, xs, tl = where[starts[c] + i]
                 nc.vector.scalar_tensor_tensor(
                     out=y[:, i, :],
                     in0=st[c]["o"][i][:],
@@ -275,11 +273,9 @@ def tile_selfattention_pa_t_kernel(tc, h_attn, x, out_w, ln_gamma, ln_beta, out)
                         )
 
         def store(c):
-            b, t0 = rows(c)
             n = SIZES[c]
             nc.sync.dma_start(
-                out=out[b].rearrange("(p t) n -> p t n", t=T)[:, t0 : t0 + n, :],
-                in_=st[c]["y"][:, 0:n, :],
+                out=out_view[:, starts[c] : starts[c] + n, :], in_=st[c]["y"][:, 0:n, :]
             )
 
         transposes(0)

@@ -170,10 +170,12 @@ def tile_selfattention_pa_t_kernel(tc, h_attn, x, out_w, ln_gamma, ln_beta, out)
             )
             st[c]["nm"] = nm
 
-        def squares(c):
+        def squares(c, lo, hi):
             y, nm = st[c]["y"], st[c]["nm"]
-            ssq = small.tile([P, 4], F32, name="ssq")
-            for i in range(SIZES[c]):
+            if lo == 0:
+                ssq = small.tile([P, 4], F32, name="ssq")
+                st[c]["ssq"] = ssq
+            for i in range(lo, min(hi, SIZES[c])):
                 junk = jpool.tile([P, E], BF16, name="junk")
                 nc.scalar.activation(
                     out=junk[:],
@@ -181,9 +183,8 @@ def tile_selfattention_pa_t_kernel(tc, h_attn, x, out_w, ln_gamma, ln_beta, out)
                     func=ACT.Square,
                     bias=nm[:, i : i + 1],
                     scale=1.0,
-                    accum_out=ssq[:, i : i + 1],
+                    accum_out=st[c]["ssq"][:, i : i + 1],
                 )
-            st[c]["ssq"] = ssq
 
         def centre_gamma(c):
             y, nm = st[c]["y"], st[c]["nm"]
@@ -315,28 +316,29 @@ def tile_selfattention_pa_t_kernel(tc, h_attn, x, out_w, ln_gamma, ln_beta, out)
                 scale_beta(k - 2)
                 if not g_tiles(k - 2):
                     store(k - 2)
-            if live(k - 3) and g_tiles(k - 3):
-                gpsimd_affine(k - 3)
-                store(k - 3)
             if live(k):
                 residual(k)
-            if live(k - 1):
-                neg_mean(k - 1)
-            if live(k + 1):
-                regroup(k + 1, 0)
-            if live(k - 1):
-                squares(k - 1)
-                centre_gamma(k - 1)
             if k == 1:
                 nc.vector.tensor_copy(out=g_sb[:], in_=g_ps[:])
                 nc.vector.tensor_copy(out=b_sb[:], in_=b_ps[:])
+            if live(k - 1):
+                neg_mean(k - 1)
+            if live(k - 2):
+                shifts(k - 2)
+            if live(k + 1):
+                regroup(k + 1, 0)
+            if live(k - 1):
+                squares(k - 1, 0, 1)
+            if live(k - 2):
+                normalise(k - 2, 0)
+                normalise(k - 2, 1)
+            if live(k - 1):
+                squares(k - 1, 1, 4)
+                centre_gamma(k - 1)
             if live(k + 1):
                 regroup(k + 1, 1)
             if live(k - 1):
                 inv_std(k - 1)
-            if live(k - 2):
-                normalise(k - 2, 0)
-            if live(k - 1):
-                shifts(k - 1)
-            if live(k - 2):
-                normalise(k - 2, 1)
+            if live(k - 2) and g_tiles(k - 2):
+                gpsimd_affine(k - 2)
+                store(k - 2)

@@ -25,7 +25,7 @@ LOADS = [(0, 4), (4, 4), (8, 8), (16, 16), (32, 32)]
 NCH = len(SIZES)
 G_LAST = 13
 G_FIRST = 0
-G_STEP = 1
+G_STEP = 2
 
 
 def g_tiles(c):
@@ -323,22 +323,19 @@ def tile_selfattention_pa_t_kernel(tc, h_attn, x, out_w, ln_gamma, ln_beta, out)
                 nc.vector.tensor_copy(out=b_sb[:], in_=b_ps[:])
             if live(k - 1):
                 neg_mean(k - 1)
-            if live(k - 2):
-                shifts(k - 2)
             if live(k + 1):
                 regroup(k + 1, 0)
-            if live(k - 1):
-                squares(k - 1, 0, 1)
             if live(k - 2):
                 normalise(k - 2, 0)
                 normalise(k - 2, 1)
             if live(k - 1):
-                squares(k - 1, 1, 4)
+                squares(k - 1, 0, 4)
                 centre_gamma(k - 1)
             if live(k + 1):
                 regroup(k + 1, 1)
             if live(k - 1):
                 inv_std(k - 1)
+                shifts(k - 1)
             if live(k - 2) and g_tiles(k - 2):
                 gpsimd_affine(k - 2)
                 store(k - 2)

@@ -112,8 +112,8 @@ def tile_selfattention_pa_t_kernel(tc, h_attn, x, out_w, ln_gamma, ln_beta, out)
             if lo < n:
                 w = min(2, n - lo)
                 nc.scalar.copy(
-                    out=st[c]["grp"][:, lo : lo + w, :],
-                    in_=st[c]["tp"][q][:, 0:w, :, :].rearrange("p i b c -> p i (b c)"),
+                    out=st[c]["grp"][:, lo : lo + w, :].rearrange("p i c -> p (i c)").bitcast(F32),
+                    in_=st[c]["tp"][q][:, 0:w, :, :].rearrange("p i b c -> p (i b c)").bitcast(F32),
                 )
 
         def quantise(c):

@@ -20,16 +20,17 @@ FLOPS = 2 * B * S * E * E
 
 MANUAL = True
 Y_BUFS = 6
-SIZES = [4] * 15 + [2, 2]
-LOADS = [(0, 4), (4, 4), (8, 8), (16, 16), (32, 32)]
+SIZES = [4,4,4,4,4,4,4,4,4,4,4,4,4,4,4,2,2]
+LOADS = [(0, 4),(4, 4),(8, 8),(16, 8),(24, 8),(32, 8),(40, 8),(48, 8),(56, 8)]
+AHEAD = 4
 NCH = len(SIZES)
 G_LAST = 13
 G_FIRST = 0
-G_STEP = 2
+G_PAT = [2,2,2,2,2,2,2,2,2,2,2,2,2,2,1,0,0]
 
 
 def g_tiles(c):
-    return 2 if G_FIRST <= c <= G_LAST else 0
+    return G_PAT[c]
 
 
 def g_norm(c):
@@ -73,22 +74,36 @@ def tile_selfattention_pa_t_kernel(tc, h_attn, x, out_w, ln_gamma, ln_beta, out)
         h_view = h_attn.rearrange("b h (q t) d -> (h q) b t d", t=T)
         x_view = x.rearrange("b s n -> (b s) n").rearrange("(m t) n -> m t n", t=T)
         out_view = out.rearrange("b s n -> (b s) n").rearrange("(m t) n -> m t n", t=T)
-        for gi, (t0, nt) in enumerate(LOADS):
+
+        hx = {}
+
+        def load_h(gi):
+            t0, nt = LOADS[gi]
             hs = inp.tile([P, B, nt, D], BF16, name="h_%d" % t0)
             nc.sync.dma_start(out=hs[:], in_=h_view[:, :, t0 : t0 + nt, :])
-            if gi == 0:
-                nc.sync.dma_start(out=w_raw[:], in_=out_w.rearrange("(h p) n -> p h n", p=P))
+            hx[gi] = hs
+
+        def load_x(gi):
+            t0, nt = LOADS[gi]
             xs = inp.tile([P, nt, E], BF16, name="x_%d" % t0)
             nc.sync.dma_start(out=xs[:], in_=x_view[:, t0 : t0 + nt, :])
-            if gi == 0:
-                nc.sync.dma_start(
-                    out=gb_row[0:1, 0:E], in_=ln_gamma.rearrange("(o n) -> o n", o=1)
-                )
-                nc.sync.dma_start(
-                    out=gb_row[0:1, E : 2 * E], in_=ln_beta.rearrange("(o n) -> o n", o=1)
-                )
             for t in range(t0, t0 + nt):
-                where[t] = (hs, xs, t - t0)
+                where[t] = (hx[gi], xs, t - t0)
+
+        def load(gi):
+            if gi < len(LOADS):
+                load_h(gi)
+                load_x(gi)
+
+        load_h(0)
+        nc.sync.dma_start(out=w_raw[:], in_=out_w.rearrange("(h p) n -> p h n", p=P))
+        load_h(1)
+        load_x(0)
+        nc.sync.dma_start(out=gb_row[0:1, 0:E], in_=ln_gamma.rearrange("(o n) -> o n", o=1))
+        nc.sync.dma_start(out=gb_row[0:1, E : 2 * E], in_=ln_beta.rearrange("(o n) -> o n", o=1))
+        load_x(1)
+        for gi in range(2, AHEAD):
+            load(gi)
 
         st = {}
 
@@ -265,13 +280,12 @@ def tile_selfattention_pa_t_kernel(tc, h_attn, x, out_w, ln_gamma, ln_beta, out)
                         op1=ALU.mult,
                     )
                 for vec, op in ((g_sb, ALU.mult), (b_sb, ALU.add)):
-                    for i in range(n - g, n, G_STEP):
-                        nc.gpsimd.tensor_tensor(
-                            out=y[:, i : i + G_STEP, :],
-                            in0=y[:, i : i + G_STEP, :],
-                            in1=vec[:].unsqueeze(1).to_broadcast([P, G_STEP, E]),
-                            op=op,
-                        )
+                    nc.gpsimd.tensor_tensor(
+                        out=y[:, n - g : n, :],
+                        in0=y[:, n - g : n, :],
+                        in1=vec[:].unsqueeze(1).to_broadcast([P, g, E]),
+                        op=op,
+                    )
 
         def store(c):
             n = SIZES[c]
@@ -302,6 +316,8 @@ def tile_selfattention_pa_t_kernel(tc, h_attn, x, out_w, ln_gamma, ln_beta, out)
             return 0 <= c < NCH
 
         for k in range(NCH + 3):
+            if k % 2 == 0:
+                load(AHEAD + k // 2)
             if live(k + 1):
                 transposes(k + 1)
             if live(k):
@@ -318,16 +334,17 @@ def tile_selfattention_pa_t_kernel(tc, h_attn, x, out_w, ln_gamma, ln_beta, out)
                     store(k - 2)
             if live(k):
                 residual(k)
-            if k == 1:
-                nc.vector.tensor_copy(out=g_sb[:], in_=g_ps[:])
-                nc.vector.tensor_copy(out=b_sb[:], in_=b_ps[:])
             if live(k - 1):
                 neg_mean(k - 1)
             if live(k + 1):
                 regroup(k + 1, 0)
+            if k == 1:
+                nc.scalar.copy(out=g_sb[:], in_=g_ps[:])
+                nc.scalar.copy(out=b_sb[:], in_=b_ps[:])
             if live(k - 2):
                 normalise(k - 2, 0)
                 normalise(k - 2, 1)
+                normalise(k - 2, 2)
             if live(k - 1):
                 squares(k - 1, 0, 4)
                 centre_gamma(k - 1)

@@ -24,6 +24,7 @@ SIZES = [4,4,4,4,4,4,4,4,4,4,4,4,4,4,4,2,2]
 LOADS = [(0, 4),(4, 4),(8, 8),(16, 8),(24, 8),(32, 8),(40, 8),(48, 8),(56, 8)]
 AHEAD = 4
 NCH = len(SIZES)
+GROUPS = [[0], [1], [2]] + [[j, j + 1] for j in range(3, 15, 2)] + [[15]]
 G_LAST = 13
 G_FIRST = 0
 G_PAT = [2,2,2,2,2,2,2,2,2,2,2,2,2,2,1,0,0]
@@ -46,7 +47,7 @@ def tile_selfattention_pa_t_kernel(tc, h_attn, x, out_w, ln_gamma, ln_beta, out)
         const = ctx.enter_context(tc.tile_pool(name="const", bufs=1))
         inp = ctx.enter_context(tc.tile_pool(name="inp", bufs=1))
         ypool = ctx.enter_context(tc.tile_pool(name="ypool", bufs=Y_BUFS))
-        gpool = ctx.enter_context(tc.tile_pool(name="gpool", bufs=3))
+        gpool = ctx.enter_context(tc.tile_pool(name="gpool", bufs=2))
         small = ctx.enter_context(tc.tile_pool(name="small", bufs=Y_BUFS + 1))
         jpool = ctx.enter_context(tc.tile_pool(name="jpool", bufs=2))
         ps_const = ctx.enter_context(tc.psum_pool(name="ps_const", bufs=1))
@@ -107,58 +108,68 @@ def tile_selfattention_pa_t_kernel(tc, h_attn, x, out_w, ln_gamma, ln_beta, out)
 
         st = {}
 
-        def transposes(c):
-            tps = []
-            for lo in range(0, SIZES[c], 2):
+        group_of = {}
+        for gi, blocks in enumerate(GROUPS):
+            for pos, j in enumerate(blocks):
+                group_of[j] = (gi, pos)
+        tps = {}
+        front = {}
+
+        def transposes(j):
+            if j >= T // 4:
+                return
+            tps[j] = []
+            for lo in (0, 2):
                 tp = ps_t.tile([P, 2, B, P], BF16, name="tp")
-                for j in range(min(2, SIZES[c] - lo)):
-                    hs, xs, tl = where[starts[c] + lo + j]
+                for i in range(2):
+                    hs, xs, tl = where[4 * j + lo + i]
                     for b in range(B):
-                        nc.tensor.transpose(out=tp[:, j, b, :], in_=hs[:, b, tl, :], identity=perm[:])
-                tps.append(tp)
-            st[c] = {"tp": tps}
+                        nc.tensor.transpose(out=tp[:, i, b, :], in_=hs[:, b, tl, :], identity=perm[:])
+                tps[j].append(tp)
 
-        def regroup(c, q):
-            n = SIZES[c]
-            if q == 0:
-                grp = gpool.tile([P, 4, P * H], BF16, align_bytes=64, name="grp")
-                st[c]["grp"] = grp
-            lo = 2 * q
-            if lo < n:
-                w = min(2, n - lo)
-                nc.scalar.copy(
-                    out=st[c]["grp"][:, lo : lo + w, :].rearrange("p i c -> p (i c)").bitcast(F32),
-                    in_=st[c]["tp"][q][:, 0:w, :, :].rearrange("p i b c -> p (i b c)").bitcast(F32),
-                )
+        def regroup(j, q):
+            if j >= T // 4:
+                return
+            gi, pos = group_of[j]
+            if pos == 0 and q == 0:
+                grp = gpool.tile([P, 8, P * H], BF16, align_bytes=64, name="grp")
+                front[gi] = {"grp": grp}
+            lo = 4 * pos + 2 * q
+            nc.scalar.copy(
+                out=front[gi]["grp"][:, lo : lo + 2, :].rearrange("p i c -> p (i c)").bitcast(F32),
+                in_=tps[j][q][:].rearrange("p i b c -> p (i b c)").bitcast(F32),
+            )
 
-        def quantise(c):
-            n = SIZES[c]
-            codes = gpool.tile([P, 4 * P], U32, align_bytes=64, name="codes")
-            scl = gpool.tile([P, 4 * P], U8, align_bytes=64, name="scl")
+        def quantise(gi):
+            n = 4 * len(GROUPS[gi])
+            codes = gpool.tile([P, 8 * P], U32, align_bytes=64, name="codes")
+            scl = gpool.tile([P, 8 * P], U8, align_bytes=64, name="scl")
             nc.vector.quantize_mx(
                 out=codes[:, 0 : n * P].bitcast(FP8X4),
                 scales=scl[:, 0 : n * P],
-                in_=st[c]["grp"][:, 0:n, :].rearrange("p i c -> p (i c)"),
+                in_=front[gi]["grp"][:, 0:n, :].rearrange("p i c -> p (i c)"),
             )
-            st[c]["codes"] = codes
-            st[c]["scl"] = scl
+            front[gi]["codes"] = codes
+            front[gi]["scl"] = scl
 
         def project(c):
-            codes, scl = st[c]["codes"], st[c]["scl"]
             banks = []
             for i in range(SIZES[c]):
+                t = starts[c] + i
+                gi, pos = group_of[t // 4]
+                j = 4 * pos + t % 4
                 o_ps = ps_o.tile([P, E], F32, name="o_ps")
                 nc.tensor.matmul_mx(
                     out=o_ps[:],
-                    lhsT=codes[:, i * P : (i + 1) * P].bitcast(FP8X4),
-                    lhsT_scale=scl[:, i * P : (i + 1) * P],
+                    lhsT=front[gi]["codes"][:, j * P : (j + 1) * P].bitcast(FP8X4),
+                    lhsT_scale=front[gi]["scl"][:, j * P : (j + 1) * P],
                     rhs=w_codes[:].bitcast(FP8X4),
                     rhs_scale=w_scl[:],
                     start=True,
                     stop=True,
                 )
                 banks.append(o_ps)
-            st[c]["o"] = banks
+            st[c] = {"o": banks}
 
         def residual(c):
             y = ypool.tile([P, 4, E], F32, name="y")
@@ -287,15 +298,27 @@ def tile_selfattention_pa_t_kernel(tc, h_attn, x, out_w, ln_gamma, ln_beta, out)
                         op=op,
                     )
 
-        def store(c):
-            n = SIZES[c]
+        def store(c, lo=0, hi=None):
+            hi = SIZES[c] if hi is None else hi
             nc.sync.dma_start(
-                out=out_view[:, starts[c] : starts[c] + n, :], in_=st[c]["y"][:, 0:n, :]
+                out=out_view[:, starts[c] + lo : starts[c] + hi, :], in_=st[c]["y"][:, lo:hi, :]
             )
 
         transposes(0)
         regroup(0, 0)
         regroup(0, 1)
+
+        def front_blocks(k):
+            if k < 2:
+                return [k + 1]
+            if k == 2:
+                return [3, 4]
+            return [k + 2]
+
+        early_done = set()
+        q_at = {}
+        for gi, blocks in enumerate(GROUPS):
+            q_at[blocks[0]] = gi
 
         w_grp = const.tile([P, E, H], BF16, align_bytes=64)
         nc.vector.tensor_copy(out=w_grp[:], in_=w_raw[:].rearrange("p h n -> p n h"))
@@ -318,10 +341,11 @@ def tile_selfattention_pa_t_kernel(tc, h_attn, x, out_w, ln_gamma, ln_beta, out)
         for k in range(NCH + 3):
             if k % 2 == 0:
                 load(AHEAD + k // 2)
-            if live(k + 1):
-                transposes(k + 1)
+            fb = front_blocks(k)
+            transposes(fb[0])
+            if k in q_at:
+                quantise(q_at[k])
             if live(k):
-                quantise(k)
                 project(k)
             if k == 0:
                 nc.tensor.matmul(out=g_ps[:], lhsT=ones[:], rhs=gb_row[:, 0:E], start=True, stop=True)
@@ -332,27 +356,37 @@ def tile_selfattention_pa_t_kernel(tc, h_attn, x, out_w, ln_gamma, ln_beta, out)
                 scale_beta(k - 2)
                 if not g_tiles(k - 2):
                     store(k - 2)
+                elif k - 2 in early_done:
+                    store(k - 2, 0, SIZES[k - 2] - g_tiles(k - 2))
             if live(k):
                 residual(k)
             if live(k - 1):
                 neg_mean(k - 1)
-            if live(k + 1):
-                regroup(k + 1, 0)
+            regroup(fb[0], 0)
             if k == 1:
                 nc.scalar.copy(out=g_sb[:], in_=g_ps[:])
                 nc.scalar.copy(out=b_sb[:], in_=b_ps[:])
-            if live(k - 2):
+            if live(k - 2) and k - 2 not in early_done:
                 normalise(k - 2, 0)
                 normalise(k - 2, 1)
-                normalise(k - 2, 2)
             if live(k - 1):
                 squares(k - 1, 0, 4)
                 centre_gamma(k - 1)
-            if live(k + 1):
-                regroup(k + 1, 1)
+            regroup(fb[0], 1)
+            for j in fb[1:]:
+                transposes(j)
             if live(k - 1):
                 inv_std(k - 1)
                 shifts(k - 1)
-            if live(k - 2) and g_tiles(k - 2):
+            for j in fb[1:]:
+                regroup(j, 0)
+                regroup(j, 1)
+            if live(k - 2) and g_tiles(k - 2) and k - 2 not in early_done:
                 gpsimd_affine(k - 2)
                 store(k - 2)
+            if k >= 3 and k in q_at and live(k - 1) and g_tiles(k - 1):
+                normalise(k - 1, 0)
+                normalise(k - 1, 1)
+                gpsimd_affine(k - 1)
+                store(k - 1, SIZES[k - 1] - g_tiles(k - 1), SIZES[k - 1])
+                early_done.add(k - 1)

@@ -21,10 +21,11 @@ FLOPS = 2 * B * S * E * E
 MANUAL = True
 Y_BUFS = 6
 SIZES = [4,4,4,4,4,4,4,4,4,4,4,4,4,4,4,2,2]
-LOADS = [(0, 4),(4, 4),(8, 8),(16, 8),(24, 8),(32, 8),(40, 8),(48, 8),(56, 8)]
-AHEAD = 4
+LOADS = [(0, 4), (4, 4), (8, 4), (12, 4)] + [(t, 8) for t in range(16, 64, 8)]
+AHEAD = 5
 NCH = len(SIZES)
-GROUPS = [[0], [1], [2]] + [[j, j + 1] for j in range(3, 15, 2)] + [[15]]
+LAST_G = 14
+GROUPS = [[0], [1]] + [[j, j + 1] for j in range(2, 16, 2)]
 G_LAST = 13
 G_FIRST = 0
 G_PAT = [2,2,2,2,2,2,2,2,2,2,2,2,2,2,1,0,0]
@@ -70,6 +71,10 @@ def tile_selfattention_pa_t_kernel(tc, h_attn, x, out_w, ln_gamma, ln_beta, out)
         warm = const.tile([P, 1], F32)
         nc.scalar.activation(out=warm[:], in_=eps[:], func=ACT.Abs_reciprocal_sqrt)
 
+        idle_ps = ps_o.tile([P, E], F32, name="o_ps")
+        for i in range(8):
+            nc.tensor.matmul(out=idle_ps[:], lhsT=ones[:], rhs=gb_row[:, 0:E], start=True, stop=True)
+
         w_raw = const.tile([P, H, E], BF16)
         where = {}
         h_view = h_attn.rearrange("b h (q t) d -> (h q) b t d", t=T)
@@ -100,11 +105,15 @@ def tile_selfattention_pa_t_kernel(tc, h_attn, x, out_w, ln_gamma, ln_beta, out)
         nc.sync.dma_start(out=w_raw[:], in_=out_w.rearrange("(h p) n -> p h n", p=P))
         load_h(1)
         load_x(0)
+        load_h(2)
         nc.sync.dma_start(out=gb_row[0:1, 0:E], in_=ln_gamma.rearrange("(o n) -> o n", o=1))
         nc.sync.dma_start(out=gb_row[0:1, E : 2 * E], in_=ln_beta.rearrange("(o n) -> o n", o=1))
         load_x(1)
-        for gi in range(2, AHEAD):
-            load(gi)
+        load_h(3)
+        load_x(2)
+        load_h(4)
+        load_x(3)
+        load_x(4)
 
         st = {}
 
@@ -275,6 +284,8 @@ def tile_selfattention_pa_t_kernel(tc, h_attn, x, out_w, ln_gamma, ln_beta, out)
                     op0=ALU.mult,
                     op1=ALU.add,
                 )
+                if c == NCH - 1:
+                    store(c, i, i + 1)
 
         def gpsimd_affine(c):
             y, nm, rstd = st[c]["y"], st[c]["nm"], st[c]["rstd"]
@@ -309,10 +320,8 @@ def tile_selfattention_pa_t_kernel(tc, h_attn, x, out_w, ln_gamma, ln_beta, out)
         regroup(0, 1)
 
         def front_blocks(k):
-            if k < 2:
-                return [k + 1]
-            if k == 2:
-                return [3, 4]
+            if k == 0:
+                return [1, 2]
             return [k + 2]
 
         early_done = set()
@@ -354,9 +363,9 @@ def tile_selfattention_pa_t_kernel(tc, h_attn, x, out_w, ln_gamma, ln_beta, out)
                 )
             if live(k - 2):
                 scale_beta(k - 2)
-                if not g_tiles(k - 2):
+                if not g_tiles(k - 2) and k - 2 < NCH - 1:
                     store(k - 2)
-                elif k - 2 in early_done:
+                elif k - 2 in early_done or k - 2 == LAST_G:
                     store(k - 2, 0, SIZES[k - 2] - g_tiles(k - 2))
             if live(k):
                 residual(k)
@@ -383,8 +392,11 @@ def tile_selfattention_pa_t_kernel(tc, h_attn, x, out_w, ln_gamma, ln_beta, out)
                 regroup(j, 1)
             if live(k - 2) and g_tiles(k - 2) and k - 2 not in early_done:
                 gpsimd_affine(k - 2)
-                store(k - 2)
-            if k >= 3 and k in q_at and live(k - 1) and g_tiles(k - 1):
+                if k - 2 == LAST_G:
+                    store(k - 2, SIZES[k - 2] - g_tiles(k - 2), SIZES[k - 2])
+                else:
+                    store(k - 2)
+            if k >= 2 and k in q_at and live(k - 1) and g_tiles(k - 1):
                 normalise(k - 1, 0)
                 normalise(k - 1, 1)
                 gpsimd_affine(k - 1)

@@ -367,7 +367,8 @@ def tile_selfattention_pa_t_kernel(tc, h_attn, x, out_w, ln_gamma, ln_beta, out)
                     store(k - 2)
                 elif k - 2 in early_done or k - 2 == LAST_G:
                     store(k - 2, 0, SIZES[k - 2] - g_tiles(k - 2))
-            if live(k):
+            late_r = k >= 2 and k in q_at
+            if live(k) and not late_r:
                 residual(k)
             if live(k - 1):
                 neg_mean(k - 1)
@@ -381,6 +382,8 @@ def tile_selfattention_pa_t_kernel(tc, h_attn, x, out_w, ln_gamma, ln_beta, out)
             if live(k - 1):
                 squares(k - 1, 0, 4)
                 centre_gamma(k - 1)
+            if live(k) and late_r:
+                residual(k)
             regroup(fb[0], 1)
             for j in fb[1:]:
                 transposes(j)

@@ -372,13 +372,16 @@ def tile_selfattention_pa_t_kernel(tc, h_attn, x, out_w, ln_gamma, ln_beta, out)
                 residual(k)
             if live(k - 1):
                 neg_mean(k - 1)
-            regroup(fb[0], 0)
+            if not late_r:
+                regroup(fb[0], 0)
             if k == 1:
                 nc.scalar.copy(out=g_sb[:], in_=g_ps[:])
                 nc.scalar.copy(out=b_sb[:], in_=b_ps[:])
             if live(k - 2) and k - 2 not in early_done:
                 normalise(k - 2, 0)
                 normalise(k - 2, 1)
+            if late_r:
+                regroup(fb[0], 0)
             if live(k - 1):
                 squares(k - 1, 0, 4)
                 centre_gamma(k - 1)

@@ -370,9 +370,11 @@ def tile_selfattention_pa_t_kernel(tc, h_attn, x, out_w, ln_gamma, ln_beta, out)
             late_r = k >= 2 and k in q_at
             if live(k) and not late_r:
                 residual(k)
+            if not late_r and k >= 3:
+                regroup(fb[0], 0)
             if live(k - 1):
                 neg_mean(k - 1)
-            if not late_r:
+            if not late_r and k < 3:
                 regroup(fb[0], 0)
             if k == 1:
                 nc.scalar.copy(out=g_sb[:], in_=g_ps[:])
@@ -380,13 +382,16 @@ def tile_selfattention_pa_t_kernel(tc, h_attn, x, out_w, ln_gamma, ln_beta, out)
             if live(k - 2) and k - 2 not in early_done:
                 normalise(k - 2, 0)
                 normalise(k - 2, 1)
-            if late_r:
-                regroup(fb[0], 0)
-            if live(k - 1):
+            if live(k - 1) and not late_r:
                 squares(k - 1, 0, 4)
                 centre_gamma(k - 1)
-            if live(k) and late_r:
-                residual(k)
+            if late_r:
+                squares(k - 1, 0, 2)
+                centre_gamma(k - 1)
+                regroup(fb[0], 0)
+                squares(k - 1, 2, 4)
+                if live(k):
+                    residual(k)
             regroup(fb[0], 1)
             for j in fb[1:]:
                 transposes(j)

@@ -52,13 +52,15 @@ def tile_selfattention_pa_t_kernel(tc, h_attn, x, out_w, ln_gamma, ln_beta, out)
         small = ctx.enter_context(tc.tile_pool(name="small", bufs=Y_BUFS + 1))
         jpool = ctx.enter_context(tc.tile_pool(name="jpool", bufs=2))
         ps_const = ctx.enter_context(tc.psum_pool(name="ps_const", bufs=1))
-        ps_t = ctx.enter_context(tc.psum_pool(name="ps_t", bufs=2))
+        ps_t = ctx.enter_context(tc.psum_pool(name="ps_t", bufs=3))
         ps_o = ctx.enter_context(tc.psum_pool(name="ps_o", bufs=4))
 
         ident = const.tile([P, P], BF16)
         make_identity(nc, ident[:])
         gb_row = const.tile([P, 2 * E], BF16)
         nc.vector.memset(gb_row[:], 0.0)
+        zeros = const.tile([P, E], BF16)
+        nc.vector.memset(zeros[:], 0.0)
         ones = const.tile([P, P], BF16)
         nc.vector.memset(ones[:], 1.0)
         eps = const.tile([P, 1], F32)
@@ -73,7 +75,7 @@ def tile_selfattention_pa_t_kernel(tc, h_attn, x, out_w, ln_gamma, ln_beta, out)
 
         idle_ps = ps_o.tile([P, E], F32, name="o_ps")
         for i in range(8):
-            nc.tensor.matmul(out=idle_ps[:], lhsT=ones[:], rhs=gb_row[:, 0:E], start=True, stop=True)
+            nc.tensor.matmul(out=idle_ps[:], lhsT=ones[:], rhs=zeros[:], start=True, stop=True)
 
         w_raw = const.tile([P, H, E], BF16)
         where = {}
@@ -103,11 +105,11 @@ def tile_selfattention_pa_t_kernel(tc, h_attn, x, out_w, ln_gamma, ln_beta, out)
 
         load_h(0)
         nc.sync.dma_start(out=w_raw[:], in_=out_w.rearrange("(h p) n -> p h n", p=P))
+        nc.sync.dma_start(out=gb_row[0:1, 0:E], in_=ln_gamma.rearrange("(o n) -> o n", o=1))
+        nc.sync.dma_start(out=gb_row[0:1, E : 2 * E], in_=ln_beta.rearrange("(o n) -> o n", o=1))
         load_h(1)
         load_x(0)
         load_h(2)
-        nc.sync.dma_start(out=gb_row[0:1, 0:E], in_=ln_gamma.rearrange("(o n) -> o n", o=1))
-        nc.sync.dma_start(out=gb_row[0:1, E : 2 * E], in_=ln_beta.rearrange("(o n) -> o n", o=1))
         load_x(1)
         load_h(3)
         load_x(2)
@@ -228,7 +230,7 @@ def tile_selfattention_pa_t_kernel(tc, h_attn, x, out_w, ln_gamma, ln_beta, out)
                     out=y[:, i, :],
                     in0=y[:, i, :],
                     scalar=nm[:, i : i + 1],
-                    in1=g_ps[:],
+                    in1=g_ps,
                     op0=ALU.add,
                     op1=ALU.mult,
                 )
@@ -280,7 +282,7 @@ def tile_selfattention_pa_t_kernel(tc, h_attn, x, out_w, ln_gamma, ln_beta, out)
                     out=y[:, i, :],
                     in0=y[:, i, :],
                     scalar=rstd[:, i : i + 1],
-                    in1=b_ps[:],
+                    in1=b_ps,
                     op0=ALU.mult,
                     op1=ALU.add,
                 )
@@ -339,8 +341,9 @@ def tile_selfattention_pa_t_kernel(tc, h_attn, x, out_w, ln_gamma, ln_beta, out)
             in_=w_grp[:].rearrange("p n h -> p (n h)"),
         )
 
-        g_ps = ps_const.tile([P, E], F32)
-        b_ps = ps_const.tile([P, E], F32)
+        gb_ps = ps_const.tile([P, 2, E], BF16)
+        g_ps = gb_ps[:, 0, :]
+        b_ps = gb_ps[:, 1, :]
         g_sb = const.tile([P, E], F32)
         b_sb = const.tile([P, E], F32)
 
@@ -352,15 +355,15 @@ def tile_selfattention_pa_t_kernel(tc, h_attn, x, out_w, ln_gamma, ln_beta, out)
                 load(AHEAD + k // 2)
             fb = front_blocks(k)
             transposes(fb[0])
+            if k == 0:
+                nc.tensor.matmul(out=g_ps, lhsT=ones[:], rhs=gb_row[:, 0:E], start=True, stop=True)
+                nc.tensor.matmul(
+                    out=b_ps, lhsT=ones[:], rhs=gb_row[:, E : 2 * E], start=True, stop=True
+                )
             if k in q_at:
                 quantise(q_at[k])
             if live(k):
                 project(k)
-            if k == 0:
-                nc.tensor.matmul(out=g_ps[:], lhsT=ones[:], rhs=gb_row[:, 0:E], start=True, stop=True)
-                nc.tensor.matmul(
-                    out=b_ps[:], lhsT=ones[:], rhs=gb_row[:, E : 2 * E], start=True, stop=True
-                )
             if live(k - 2):
                 scale_beta(k - 2)
                 if not g_tiles(k - 2) and k - 2 < NCH - 1:
@@ -376,9 +379,10 @@ def tile_selfattention_pa_t_kernel(tc, h_attn, x, out_w, ln_gamma, ln_beta, out)
                 neg_mean(k - 1)
             if not late_r and k < 3:
                 regroup(fb[0], 0)
-            if k == 1:
-                nc.scalar.copy(out=g_sb[:], in_=g_ps[:])
-                nc.scalar.copy(out=b_sb[:], in_=b_ps[:])
+            if k == 0:
+                regroup(fb[0], 1)
+                nc.scalar.copy(out=g_sb[:], in_=g_ps)
+                nc.scalar.copy(out=b_sb[:], in_=b_ps)
             if live(k - 2) and k - 2 not in early_done:
                 normalise(k - 2, 0)
                 normalise(k - 2, 1)
@@ -392,7 +396,8 @@ def tile_selfattention_pa_t_kernel(tc, h_attn, x, out_w, ln_gamma, ln_beta, out)
                 squares(k - 1, 2, 4)
                 if live(k):
                     residual(k)
-            regroup(fb[0], 1)
+            if k > 0:
+                regroup(fb[0], 1)
             for j in fb[1:]:
                 transposes(j)
             if live(k - 1):

@@ -18,38 +18,32 @@ T = B * S // P
 LN_EPS = 1e-6
 FLOPS = 2 * B * S * E * E
 
-MANUAL = True
-Y_BUFS = 6
-SIZES = [4,4,4,4,4,4,4,4,4,4,4,4,4,4,4,2,2]
+NCH = T // 4
 LOADS = [(0, 4), (4, 4), (8, 4), (12, 4)] + [(t, 8) for t in range(16, 64, 8)]
-AHEAD = 5
-NCH = len(SIZES)
-LAST_G = 14
-GROUPS = [[0], [1]] + [[j, j + 1] for j in range(2, 16, 2)]
-G_LAST = 13
-G_FIRST = 0
-G_PAT = [2,2,2,2,2,2,2,2,2,2,2,2,2,2,1,0,0]
+GROUPS = [[0], [1]] + [[j, j + 1] for j in range(2, NCH, 2)]
+LOAD_AT = {0: 5, 2: 6, 4: 7, 6: 8, 8: 9}
 
 
-def g_tiles(c):
-    return G_PAT[c]
+def on_gpsimd(c):
+    if c == 0:
+        return [1, 2, 3]
+    return [2, 3] if c < NCH - 2 else []
 
 
-def g_norm(c):
-    return 0
+def on_vector(c):
+    return [i for i in range(4) if i not in on_gpsimd(c)]
 
 
 def tile_selfattention_pa_t_kernel(tc, h_attn, x, out_w, ln_gamma, ln_beta, out):
     nc = tc.nc
-    starts = [sum(SIZES[:c]) for c in range(NCH)]
     with ExitStack() as ctx:
-        if MANUAL:
-            ctx.enter_context(tc.manual_schedule())
+        ctx.enter_context(tc.manual_schedule())
         const = ctx.enter_context(tc.tile_pool(name="const", bufs=1))
         inp = ctx.enter_context(tc.tile_pool(name="inp", bufs=1))
-        ypool = ctx.enter_context(tc.tile_pool(name="ypool", bufs=Y_BUFS))
+        yvpool = ctx.enter_context(tc.tile_pool(name="yvpool", bufs=5))
+        ygpool = ctx.enter_context(tc.tile_pool(name="ygpool", bufs=4))
         gpool = ctx.enter_context(tc.tile_pool(name="gpool", bufs=2))
-        small = ctx.enter_context(tc.tile_pool(name="small", bufs=Y_BUFS + 1))
+        small = ctx.enter_context(tc.tile_pool(name="small", bufs=7))
         jpool = ctx.enter_context(tc.tile_pool(name="jpool", bufs=2))
         ps_const = ctx.enter_context(tc.psum_pool(name="ps_const", bufs=1))
         ps_t = ctx.enter_context(tc.psum_pool(name="ps_t", bufs=3))
@@ -118,17 +112,14 @@ def tile_selfattention_pa_t_kernel(tc, h_attn, x, out_w, ln_gamma, ln_beta, out)
         load_x(4)
 
         st = {}
-
         group_of = {}
-        for gi, blocks in enumerate(GROUPS):
-            for pos, j in enumerate(blocks):
+        for gi, chunks in enumerate(GROUPS):
+            for pos, j in enumerate(chunks):
                 group_of[j] = (gi, pos)
         tps = {}
         front = {}
 
         def transposes(j):
-            if j >= T // 4:
-                return
             tps[j] = []
             for lo in (0, 2):
                 tp = ps_t.tile([P, 2, B, P], BF16, name="tp")
@@ -138,15 +129,13 @@ def tile_selfattention_pa_t_kernel(tc, h_attn, x, out_w, ln_gamma, ln_beta, out)
                         nc.tensor.transpose(out=tp[:, i, b, :], in_=hs[:, b, tl, :], identity=perm[:])
                 tps[j].append(tp)
 
-        def regroup(j, q):
-            if j >= T // 4:
-                return
+        def regroup(j, q, copy=nc.scalar.copy):
             gi, pos = group_of[j]
             if pos == 0 and q == 0:
                 grp = gpool.tile([P, 8, P * H], BF16, align_bytes=64, name="grp")
                 front[gi] = {"grp": grp}
             lo = 4 * pos + 2 * q
-            nc.scalar.copy(
+            copy(
                 out=front[gi]["grp"][:, lo : lo + 2, :].rearrange("p i c -> p (i c)").bitcast(F32),
                 in_=tps[j][q][:].rearrange("p i b c -> p (i b c)").bitcast(F32),
             )
@@ -164,11 +153,10 @@ def tile_selfattention_pa_t_kernel(tc, h_attn, x, out_w, ln_gamma, ln_beta, out)
             front[gi]["scl"] = scl
 
         def project(c):
+            gi, pos = group_of[c]
             banks = []
-            for i in range(SIZES[c]):
-                t = starts[c] + i
-                gi, pos = group_of[t // 4]
-                j = 4 * pos + t % 4
+            for i in range(4):
+                j = 4 * pos + i
                 o_ps = ps_o.tile([P, E], F32, name="o_ps")
                 nc.tensor.matmul_mx(
                     out=o_ps[:],
@@ -182,154 +170,124 @@ def tile_selfattention_pa_t_kernel(tc, h_attn, x, out_w, ln_gamma, ln_beta, out)
                 banks.append(o_ps)
             st[c] = {"o": banks}
 
-        def residual(c):
-            y = ypool.tile([P, 4, E], F32, name="y")
-            sums = small.tile([P, 4], F32, name="sums")
-            for i in range(SIZES[c]):
-                hs, xs, tl = where[starts[c] + i]
+        def ya(c, i):
+            if c == 0:
+                return st[c]["yg"][:, i, :]
+            if i < 2:
+                return st[c]["yv"][:, i, :]
+            return st[c]["yg"][:, (i - 2 if c % 2 else i), :]
+
+        def residual(c, lo=0, hi=4):
+            if lo == 0:
+                new_y(c)
+            for i in range(lo, hi):
+                hs, xs, tl = where[4 * c + i]
                 nc.vector.scalar_tensor_tensor(
-                    out=y[:, i, :],
+                    out=ya(c, i),
                     in0=st[c]["o"][i][:],
                     scalar=0.0,
                     in1=xs[:, tl, :],
                     op0=ALU.add,
                     op1=ALU.add,
-                    accum_out=sums[:, i : i + 1],
+                    accum_out=st[c]["sums"][:, i : i + 1],
                 )
-            st[c]["y"] = y
+
+        def new_y(c):
+            if c > 0:
+                yv = yvpool.tile([P, 2, E], F32, name="yv")
+                st[c]["yv"] = yv
+            if c == 0 or c % 2:
+                yg = ygpool.tile([P, 4, E], F32, name="yg")
+                st[c]["yg"] = yg
+            else:
+                st[c]["yg"] = st[c - 1]["yg"]
+            sums = small.tile([P, 4], F32, name="sums")
             st[c]["sums"] = sums
 
-        def neg_mean(c):
-            n = SIZES[c]
-            nm = small.tile([P, 4], F32, name="nm")
-            nc.scalar.activation(
-                out=nm[:, 0:n], in_=st[c]["sums"][:, 0:n], func=ACT.Copy, scale=-1.0 / E
-            )
-            st[c]["nm"] = nm
-
-        def squares(c, lo, hi):
-            y, nm = st[c]["y"], st[c]["nm"]
+        def neg_mean(c, lo=0, hi=4):
             if lo == 0:
+                nm = small.tile([P, 4], F32, name="nm")
                 ssq = small.tile([P, 4], F32, name="ssq")
+                rstd = small.tile([P, 4], F32, name="rstd")
+                nmr = small.tile([P, 4], F32, name="nmr")
+                st[c]["nm"] = nm
                 st[c]["ssq"] = ssq
-            for i in range(lo, min(hi, SIZES[c])):
+                st[c]["rstd"] = rstd
+                st[c]["nmr"] = nmr
+            nc.scalar.activation(out=st[c]["nm"][:, lo:hi], in_=st[c]["sums"][:, lo:hi], func=ACT.Copy, scale=-1.0 / E)
+
+        def squares(c, tiles):
+            for i in tiles:
                 junk = jpool.tile([P, E], BF16, name="junk")
                 nc.scalar.activation(
                     out=junk[:],
-                    in_=y[:, i, :],
+                    in_=ya(c, i),
                     func=ACT.Square,
-                    bias=nm[:, i : i + 1],
+                    bias=st[c]["nm"][:, i : i + 1],
                     scale=1.0,
                     accum_out=st[c]["ssq"][:, i : i + 1],
                 )
 
-        def centre_gamma(c):
-            y, nm = st[c]["y"], st[c]["nm"]
-            for i in range(SIZES[c] - g_tiles(c)):
-                nc.vector.scalar_tensor_tensor(
-                    out=y[:, i, :],
-                    in0=y[:, i, :],
-                    scalar=nm[:, i : i + 1],
-                    in1=g_ps,
-                    op0=ALU.add,
-                    op1=ALU.mult,
-                )
-
-        def inv_std(c):
-            n = SIZES[c]
-            rstd = small.tile([P, 4], F32, name="rstd")
+        def inv_std(c, lo=0, hi=4):
             nc.scalar.activation(
-                out=rstd[:, 0:n],
-                in_=st[c]["ssq"][:, 0:n],
+                out=st[c]["rstd"][:, lo:hi],
+                in_=st[c]["ssq"][:, lo:hi],
                 func=ACT.Abs_reciprocal_sqrt,
                 bias=eps[:, 0:1],
                 scale=1.0 / E,
             )
-            st[c]["rstd"] = rstd
 
-        def on_scalar(c):
-            return list(range(SIZES[c] - g_tiles(c), SIZES[c] - g_norm(c))) if g_tiles(c) else []
+        def centre_gamma(c, tiles=None):
+            for i in on_vector(c) if tiles is None else tiles:
+                nc.vector.scalar_tensor_tensor(
+                    out=ya(c, i), in0=ya(c, i), scalar=st[c]["nm"][:, i : i + 1], in1=g_ps, op0=ALU.add, op1=ALU.mult
+                )
+
+        def scale_beta(c, tiles=None):
+            for i in on_vector(c) if tiles is None else tiles:
+                nc.vector.scalar_tensor_tensor(
+                    out=ya(c, i), in0=ya(c, i), scalar=st[c]["rstd"][:, i : i + 1], in1=b_ps, op0=ALU.mult, op1=ALU.add
+                )
 
         def shifts(c):
-            nm, rstd = st[c]["nm"], st[c]["rstd"]
-            if on_scalar(c):
-                nmr = small.tile([P, 4], F32, name="nmr")
-                st[c]["nmr"] = nmr
-                for i in on_scalar(c):
-                    nc.scalar.activation(
-                        out=nmr[:, i : i + 1],
-                        in_=nm[:, i : i + 1],
-                        func=ACT.Copy,
-                        scale=rstd[:, i : i + 1],
-                    )
-
-        def normalise(c, j):
-            if j < len(on_scalar(c)):
-                i = on_scalar(c)[j]
-                y = st[c]["y"]
+            for i in on_gpsimd(c):
                 nc.scalar.activation(
-                    out=y[:, i, :],
-                    in_=y[:, i, :],
+                    out=st[c]["nmr"][:, i : i + 1],
+                    in_=st[c]["nm"][:, i : i + 1],
+                    func=ACT.Copy,
+                    scale=st[c]["rstd"][:, i : i + 1],
+                )
+
+        def normalise(c, tiles=(2, 3)):
+            for i in tiles:
+                nc.scalar.activation(
+                    out=ya(c, i),
+                    in_=ya(c, i),
                     func=ACT.Identity,
                     bias=st[c]["nmr"][:, i : i + 1],
                     scale=st[c]["rstd"][:, i : i + 1],
                 )
 
-        def scale_beta(c):
-            y, rstd = st[c]["y"], st[c]["rstd"]
-            for i in range(SIZES[c] - g_tiles(c)):
-                nc.vector.scalar_tensor_tensor(
-                    out=y[:, i, :],
-                    in0=y[:, i, :],
-                    scalar=rstd[:, i : i + 1],
-                    in1=b_ps,
-                    op0=ALU.mult,
-                    op1=ALU.add,
-                )
-                if c == NCH - 1:
-                    store(c, i, i + 1)
+        def affine(c, n, lo=None):
+            lo = lo if lo is not None else 0
+            yg = st[c]["yg"][:, lo : lo + n, :]
+            for vec, op in ((g_sb, ALU.mult), (b_sb, ALU.add)):
+                nc.gpsimd.tensor_tensor(out=yg, in0=yg, in1=vec[:].unsqueeze(1).to_broadcast([P, n, E]), op=op)
 
-        def gpsimd_affine(c):
-            y, nm, rstd = st[c]["y"], st[c]["nm"], st[c]["rstd"]
-            n = SIZES[c]
-            g = g_tiles(c)
-            if g:
-                for i in range(n - g_norm(c), n):
-                    nc.gpsimd.tensor_scalar(
-                        out=y[:, i, :],
-                        in0=y[:, i, :],
-                        scalar1=nm[:, i : i + 1],
-                        scalar2=rstd[:, i : i + 1],
-                        op0=ALU.add,
-                        op1=ALU.mult,
-                    )
-                for vec, op in ((g_sb, ALU.mult), (b_sb, ALU.add)):
-                    nc.gpsimd.tensor_tensor(
-                        out=y[:, n - g : n, :],
-                        in0=y[:, n - g : n, :],
-                        in1=vec[:].unsqueeze(1).to_broadcast([P, g, E]),
-                        op=op,
-                    )
+        def store_v(c):
+            if c > 0:
+                nc.sync.dma_start(out=out_view[:, 4 * c : 4 * c + 2, :], in_=st[c]["yv"][:])
 
-        def store(c, lo=0, hi=None):
-            hi = SIZES[c] if hi is None else hi
-            nc.sync.dma_start(
-                out=out_view[:, starts[c] + lo : starts[c] + hi, :], in_=st[c]["y"][:, lo:hi, :]
-            )
+        def store_g(c):
+            if c == 0:
+                nc.sync.dma_start(out=out_view[:, 0:4, :], in_=st[c]["yg"][:])
+                return
+            lo = 0 if c % 2 else 2
+            nc.sync.dma_start(out=out_view[:, 4 * c + 2 : 4 * c + 4, :], in_=st[c]["yg"][:, lo : lo + 2, :])
 
         transposes(0)
         regroup(0, 0)
         regroup(0, 1)
-
-        def front_blocks(k):
-            if k == 0:
-                return [1, 2]
-            return [k + 2]
-
-        early_done = set()
-        q_at = {}
-        for gi, blocks in enumerate(GROUPS):
-            q_at[blocks[0]] = gi
 
         w_grp = const.tile([P, E, H], BF16, align_bytes=64)
         nc.vector.tensor_copy(out=w_grp[:], in_=w_raw[:].rearrange("p h n -> p n h"))
@@ -346,75 +304,104 @@ def tile_selfattention_pa_t_kernel(tc, h_attn, x, out_w, ln_gamma, ln_beta, out)
         b_ps = gb_ps[:, 1, :]
         g_sb = const.tile([P, E], F32)
         b_sb = const.tile([P, E], F32)
+        stores = {}
 
-        def live(c):
-            return 0 <= c < NCH
-
-        for k in range(NCH + 3):
-            if k % 2 == 0:
-                load(AHEAD + k // 2)
-            fb = front_blocks(k)
-            transposes(fb[0])
+        for k in range(NCH - 1):
+            if k in LOAD_AT:
+                load(LOAD_AT[k])
+            for c in stores.get(k, []):
+                store_g(c)
+            fb = [1, 2] if k == 0 else [k + 2] if k + 2 < NCH else []
+            late = k >= 2 and k % 2 == 0
+            if fb:
+                transposes(fb[0])
             if k == 0:
                 nc.tensor.matmul(out=g_ps, lhsT=ones[:], rhs=gb_row[:, 0:E], start=True, stop=True)
-                nc.tensor.matmul(
-                    out=b_ps, lhsT=ones[:], rhs=gb_row[:, E : 2 * E], start=True, stop=True
-                )
-            if k in q_at:
-                quantise(q_at[k])
-            if live(k):
-                project(k)
-            if live(k - 2):
+                nc.tensor.matmul(out=b_ps, lhsT=ones[:], rhs=gb_row[:, E : 2 * E], start=True, stop=True)
+            if k < 2 or late:
+                quantise(k if k < 2 else k // 2 + 1)
+            project(k)
+            if k >= 2:
                 scale_beta(k - 2)
-                if not g_tiles(k - 2) and k - 2 < NCH - 1:
-                    store(k - 2)
-                elif k - 2 in early_done or k - 2 == LAST_G:
-                    store(k - 2, 0, SIZES[k - 2] - g_tiles(k - 2))
-            late_r = k >= 2 and k in q_at
-            if live(k) and not late_r:
+                store_v(k - 2)
+            if k == 0:
+                regroup(1, 0)
+                regroup(1, 1, nc.vector.tensor_copy)
+            if k == 1:
+                regroup(2, 1, nc.vector.tensor_copy)
+            if not late:
                 residual(k)
-            if not late_r and k >= 3:
+            if fb and not late and k >= 3:
                 regroup(fb[0], 0)
-            if live(k - 1):
+            if k >= 1:
                 neg_mean(k - 1)
-            if not late_r and k < 3:
+            if k == 1:
                 regroup(fb[0], 0)
             if k == 0:
-                regroup(fb[0], 1)
                 nc.scalar.copy(out=g_sb[:], in_=g_ps)
                 nc.scalar.copy(out=b_sb[:], in_=b_ps)
-            if live(k - 2) and k - 2 not in early_done:
-                normalise(k - 2, 0)
-                normalise(k - 2, 1)
-            if live(k - 1) and not late_r:
-                squares(k - 1, 0, 4)
+            if k >= 2:
+                normalise(k - 2)
+            if late:
+                if k == 2:
+                    affine(0, 2, 2)
+                else:
+                    affine(k - 2, 4)
+                stores[k + 2] = [0] if k == 2 else [k - 3, k - 2]
+                squares(k - 1, [0, 1])
                 centre_gamma(k - 1)
-            if late_r:
-                squares(k - 1, 0, 2)
+                if fb:
+                    regroup(fb[0], 0)
+                squares(k - 1, [2, 3])
+                residual(k)
+            elif k >= 1:
+                squares(k - 1, [0, 1, 2, 3])
                 centre_gamma(k - 1)
-                regroup(fb[0], 0)
-                squares(k - 1, 2, 4)
-                if live(k):
-                    residual(k)
-            if k > 0:
+            if fb and k > 0:
                 regroup(fb[0], 1)
-            for j in fb[1:]:
-                transposes(j)
-            if live(k - 1):
+            if k >= 1:
                 inv_std(k - 1)
                 shifts(k - 1)
+            if k == 2:
+                normalise(0, (1,))
+                affine(0, 1, 1)
             for j in fb[1:]:
+                transposes(j)
                 regroup(j, 0)
-                regroup(j, 1)
-            if live(k - 2) and g_tiles(k - 2) and k - 2 not in early_done:
-                gpsimd_affine(k - 2)
-                if k - 2 == LAST_G:
-                    store(k - 2, SIZES[k - 2] - g_tiles(k - 2), SIZES[k - 2])
-                else:
-                    store(k - 2)
-            if k >= 2 and k in q_at and live(k - 1) and g_tiles(k - 1):
-                normalise(k - 1, 0)
-                normalise(k - 1, 1)
-                gpsimd_affine(k - 1)
-                store(k - 1, SIZES[k - 1] - g_tiles(k - 1), SIZES[k - 1])
-                early_done.add(k - 1)
+
+        def store_rows(c, lo, hi):
+            y = st[c]["yv"][:, lo:hi, :] if hi <= 2 else st[c]["yg"][:, (lo - 2 if c % 2 else lo) : (hi - 2 if c % 2 else hi), :]
+            nc.sync.dma_start(out=out_view[:, 4 * c + lo : 4 * c + hi, :], in_=y)
+
+        e = NCH - 1
+        project(e)
+        scale_beta(e - 2)
+        store_v(e - 2)
+        residual(e, 0, 2)
+        neg_mean(e - 1)
+        normalise(e - 2)
+        affine(e - 2, 2)
+        squares(e - 1, [0, 1, 2, 3])
+        centre_gamma(e - 1)
+        inv_std(e - 1)
+        scale_beta(e - 1)
+        for c in stores[e + 1]:
+            store_g(c)
+        store_rows(e - 1, 0, 2)
+        store_rows(e - 1, 2, 4)
+        residual(e, 2, 4)
+        neg_mean(e, 0, 2)
+        squares(e, [0, 1])
+        centre_gamma(e, [0, 1])
+        inv_std(e, 0, 2)
+        neg_mean(e, 2, 4)
+        squares(e, [2, 3])
+        store_g(e - 2)
+        scale_beta(e, [0, 1])
+        store_rows(e, 0, 2)
+        centre_gamma(e, [2, 3])
+        inv_std(e, 2, 4)
+        scale_beta(e, [2])
+        store_rows(e, 2, 3)
+        scale_beta(e, [3])
+        store_rows(e, 3, 4)

@@ -27,7 +27,7 @@ LOAD_AT = {0: 5, 2: 6, 4: 7, 6: 8, 8: 9}
 def on_gpsimd(c):
     if c == 0:
         return [1, 2, 3]
-    return [2, 3] if c < NCH - 2 else []
+    return [2, 3] if c < NCH - 2 else [2] if c == NCH - 2 else []
 
 
 def on_vector(c):
@@ -250,7 +250,7 @@ def tile_selfattention_pa_t_kernel(tc, h_attn, x, out_w, ln_gamma, ln_beta, out)
                 )
 
         def shifts(c):
-            for i in on_gpsimd(c):
+            for i in on_gpsimd(c)[-2:]:
                 nc.scalar.activation(
                     out=st[c]["nmr"][:, i : i + 1],
                     in_=st[c]["nm"][:, i : i + 1],
@@ -333,15 +333,16 @@ def tile_selfattention_pa_t_kernel(tc, h_attn, x, out_w, ln_gamma, ln_beta, out)
                 residual(k)
             if fb and not late and k >= 3:
                 regroup(fb[0], 0)
+                regroup(fb[0], 1)
             if k >= 1:
-                neg_mean(k - 1)
+                neg_mean(k - 1, 2 if k == 1 else 0)
             if k == 1:
                 regroup(fb[0], 0)
             if k == 0:
                 nc.scalar.copy(out=g_sb[:], in_=g_ps)
                 nc.scalar.copy(out=b_sb[:], in_=b_ps)
             if k >= 2:
-                normalise(k - 2)
+                normalise(k - 2, (3,) if k >= 4 and late else (2, 3))
             if late:
                 if k == 2:
                     affine(0, 2, 2)
@@ -354,20 +355,40 @@ def tile_selfattention_pa_t_kernel(tc, h_attn, x, out_w, ln_gamma, ln_beta, out)
                     regroup(fb[0], 0)
                 squares(k - 1, [2, 3])
                 residual(k)
-            elif k >= 1:
-                squares(k - 1, [0, 1, 2, 3])
+            elif k >= 3:
+                squares(k - 1, [2, 3, 0])
+                inv_std(k - 1, 2, 4)
+                squares(k - 1, [1])
+                shifts(k - 1)
                 centre_gamma(k - 1)
-            if fb and k > 0:
+            elif k == 1:
+                squares(0, [2, 3])
+                centre_gamma(0)
+            if fb and (k == 1 or late):
                 regroup(fb[0], 1)
-            if k >= 1:
+            if k >= 3 and not late:
+                inv_std(k - 1, 0, 2)
+                normalise(k - 1, (2,))
+            elif k >= 1:
                 inv_std(k - 1)
                 shifts(k - 1)
             if k == 2:
-                normalise(0, (1,))
+                one = ya(0, 1)
+                nc.gpsimd.tensor_scalar(
+                    out=one,
+                    in0=one,
+                    scalar1=st[0]["nm"][:, 1:2],
+                    scalar2=st[0]["rstd"][:, 1:2],
+                    op0=ALU.add,
+                    op1=ALU.mult,
+                )
                 affine(0, 1, 1)
             for j in fb[1:]:
                 transposes(j)
                 regroup(j, 0)
+            if k == 0:
+                neg_mean(0, 0, 2)
+                squares(0, [0, 1])
 
         def store_rows(c, lo, hi):
             y = st[c]["yv"][:, lo:hi, :] if hi <= 2 else st[c]["yg"][:, (lo - 2 if c % 2 else lo) : (hi - 2 if c % 2 else hi), :]
@@ -381,14 +402,18 @@ def tile_selfattention_pa_t_kernel(tc, h_attn, x, out_w, ln_gamma, ln_beta, out)
         neg_mean(e - 1)
         normalise(e - 2)
         affine(e - 2, 2)
-        squares(e - 1, [0, 1, 2, 3])
+        squares(e - 1, [0, 1, 3, 2])
         centre_gamma(e - 1)
         inv_std(e - 1)
+        shifts(e - 1)
         scale_beta(e - 1)
         for c in stores[e + 1]:
             store_g(c)
         store_rows(e - 1, 0, 2)
-        store_rows(e - 1, 2, 4)
+        store_rows(e - 1, 3, 4)
+        normalise(e - 1, on_gpsimd(e - 1))
+        last = ya(e - 1, 2)
+        nc.gpsimd.tensor_tensor(out=last, in0=last, in1=g_sb[:], op=ALU.mult)
         residual(e, 2, 4)
         neg_mean(e, 0, 2)
         squares(e, [0, 1])
@@ -403,5 +428,7 @@ def tile_selfattention_pa_t_kernel(tc, h_attn, x, out_w, ln_gamma, ln_beta, out)
         inv_std(e, 2, 4)
         scale_beta(e, [2])
         store_rows(e, 2, 3)
+        nc.vector.tensor_tensor(out=last, in0=last, in1=b_ps, op=ALU.add)
+        store_rows(e - 1, 2, 3)
         scale_beta(e, [3])
         store_rows(e, 3, 4)

@@ -27,7 +27,7 @@ LOAD_AT = {0: 5, 2: 6, 4: 7, 6: 8, 8: 9}
 def on_gpsimd(c):
     if c == 0:
         return [1, 2, 3]
-    return [2, 3] if c < NCH - 2 else [2] if c == NCH - 2 else []
+    return [2, 3] if c < NCH - 2 else []
 
 
 def on_vector(c):
@@ -342,7 +342,7 @@ def tile_selfattention_pa_t_kernel(tc, h_attn, x, out_w, ln_gamma, ln_beta, out)
                 nc.scalar.copy(out=g_sb[:], in_=g_ps)
                 nc.scalar.copy(out=b_sb[:], in_=b_ps)
             if k >= 2:
-                normalise(k - 2, (3,) if k >= 4 and late else (2, 3))
+                normalise(k - 2)
             if late:
                 if k == 2:
                     affine(0, 2, 2)
@@ -368,7 +368,6 @@ def tile_selfattention_pa_t_kernel(tc, h_attn, x, out_w, ln_gamma, ln_beta, out)
                 regroup(fb[0], 1)
             if k >= 3 and not late:
                 inv_std(k - 1, 0, 2)
-                normalise(k - 1, (2,))
             elif k >= 1:
                 inv_std(k - 1)
                 shifts(k - 1)
@@ -402,18 +401,14 @@ def tile_selfattention_pa_t_kernel(tc, h_attn, x, out_w, ln_gamma, ln_beta, out)
         neg_mean(e - 1)
         normalise(e - 2)
         affine(e - 2, 2)
-        squares(e - 1, [0, 1, 3, 2])
+        squares(e - 1, [0, 1, 2, 3])
         centre_gamma(e - 1)
         inv_std(e - 1)
-        shifts(e - 1)
         scale_beta(e - 1)
         for c in stores[e + 1]:
             store_g(c)
         store_rows(e - 1, 0, 2)
-        store_rows(e - 1, 3, 4)
-        normalise(e - 1, on_gpsimd(e - 1))
-        last = ya(e - 1, 2)
-        nc.gpsimd.tensor_tensor(out=last, in0=last, in1=g_sb[:], op=ALU.mult)
+        store_rows(e - 1, 2, 4)
         residual(e, 2, 4)
         neg_mean(e, 0, 2)
         squares(e, [0, 1])
@@ -428,7 +423,5 @@ def tile_selfattention_pa_t_kernel(tc, h_attn, x, out_w, ln_gamma, ln_beta, out)
         inv_std(e, 2, 4)
         scale_beta(e, [2])
         store_rows(e, 2, 3)
-        nc.vector.tensor_tensor(out=last, in0=last, in1=b_ps, op=ALU.add)
-        store_rows(e - 1, 2, 3)
         scale_beta(e, [3])
         store_rows(e, 3, 4)

@@ -104,10 +104,10 @@ def tile_selfattention_pa_t_kernel(tc, h_attn, x, out_w, ln_gamma, ln_beta, out)
         load_h(1)
         load_x(0)
         load_h(2)
-        load_x(1)
         load_h(3)
-        load_x(2)
+        load_x(1)
         load_h(4)
+        load_x(2)
         load_x(3)
         load_x(4)
 

from contextlib import ExitStack

import concourse.mybir as mybir
from concourse.masks import make_identity

FP8X4 = mybir.dt.float8_e4m3fn_x4
BF16 = mybir.dt.bfloat16
F32 = mybir.dt.float32
U32 = mybir.dt.uint32
U8 = mybir.dt.uint8
ALU = mybir.AluOpType
ACT = mybir.ActivationFunctionType

B, H, S, D = 4, 4, 2048, 128
E = H * D
P = 128
T = B * S // P
LN_EPS = 1e-6
FLOPS = 2 * B * S * E * E

NCH = T // 4
LOADS = [(0, 4), (4, 4), (8, 4), (12, 4)] + [(t, 8) for t in range(16, 64, 8)]
GROUPS = [[0], [1]] + [[j, j + 1] for j in range(2, NCH, 2)]
LOAD_AT = {0: 5, 2: 6, 4: 7, 6: 8, 8: 9}


def on_gpsimd(c):
    if c == 0:
        return [1, 2, 3]
    return [2, 3] if c < NCH - 2 else []


def on_vector(c):
    return [i for i in range(4) if i not in on_gpsimd(c)]


def tile_selfattention_pa_t_kernel(tc, h_attn, x, out_w, ln_gamma, ln_beta, out):
    nc = tc.nc
    with ExitStack() as ctx:
        ctx.enter_context(tc.manual_schedule())
        const = ctx.enter_context(tc.tile_pool(name="const", bufs=1))
        inp = ctx.enter_context(tc.tile_pool(name="inp", bufs=1))
        yvpool = ctx.enter_context(tc.tile_pool(name="yvpool", bufs=5))
        ygpool = ctx.enter_context(tc.tile_pool(name="ygpool", bufs=4))
        gpool = ctx.enter_context(tc.tile_pool(name="gpool", bufs=2))
        small = ctx.enter_context(tc.tile_pool(name="small", bufs=7))
        jpool = ctx.enter_context(tc.tile_pool(name="jpool", bufs=2))
        ps_const = ctx.enter_context(tc.psum_pool(name="ps_const", bufs=1))
        ps_t = ctx.enter_context(tc.psum_pool(name="ps_t", bufs=3))
        ps_o = ctx.enter_context(tc.psum_pool(name="ps_o", bufs=4))

        ident = const.tile([P, P], BF16)
        make_identity(nc, ident[:])
        gb_row = const.tile([P, 2 * E], BF16)
        nc.vector.memset(gb_row[:], 0.0)
        zeros = const.tile([P, E], BF16)
        nc.vector.memset(zeros[:], 0.0)
        ones = const.tile([P, P], BF16)
        nc.vector.memset(ones[:], 1.0)
        eps = const.tile([P, 1], F32)
        nc.vector.memset(eps[:], LN_EPS)
        perm = const.tile([P, P], BF16)
        nc.vector.tensor_copy(
            out=perm[:].rearrange("p (q h) -> p q h", h=H),
            in_=ident[:].rearrange("p (h q) -> p q h", h=H),
        )
        warm = const.tile([P, 1], F32)
        nc.scalar.activation(out=warm[:], in_=eps[:], func=ACT.Abs_reciprocal_sqrt)

        idle_ps = ps_o.tile([P, E], F32, name="o_ps")
        for i in range(8):
            nc.tensor.matmul(out=idle_ps[:], lhsT=ones[:], rhs=zeros[:], start=True, stop=True)

        w_raw = const.tile([P, H, E], BF16)
        where = {}
        h_view = h_attn.rearrange("b h (q t) d -> (h q) b t d", t=T)
        x_view = x.rearrange("b s n -> (b s) n").rearrange("(m t) n -> m t n", t=T)
        out_view = out.rearrange("b s n -> (b s) n").rearrange("(m t) n -> m t n", t=T)

        hx = {}

        def load_h(gi):
            t0, nt = LOADS[gi]
            hs = inp.tile([P, B, nt, D], BF16, name="h_%d" % t0)
            nc.sync.dma_start(out=hs[:], in_=h_view[:, :, t0 : t0 + nt, :])
            hx[gi] = hs

        def load_x(gi):
            t0, nt = LOADS[gi]
            xs = inp.tile([P, nt, E], BF16, name="x_%d" % t0)
            nc.sync.dma_start(out=xs[:], in_=x_view[:, t0 : t0 + nt, :])
            for t in range(t0, t0 + nt):
                where[t] = (hx[gi], xs, t - t0)

        def load(gi):
            if gi < len(LOADS):
                load_h(gi)
                load_x(gi)

        load_h(0)
        nc.sync.dma_start(out=w_raw[:], in_=out_w.rearrange("(h p) n -> p h n", p=P))
        nc.sync.dma_start(out=gb_row[0:1, 0:E], in_=ln_gamma.rearrange("(o n) -> o n", o=1))
        nc.sync.dma_start(out=gb_row[0:1, E : 2 * E], in_=ln_beta.rearrange("(o n) -> o n", o=1))
        load_h(1)
        load_x(0)
        load_h(2)
        load_h(3)
        load_x(1)
        load_h(4)
        load_x(2)
        load_x(3)
        load_x(4)

        st = {}
        group_of = {}
        for gi, chunks in enumerate(GROUPS):
            for pos, j in enumerate(chunks):
                group_of[j] = (gi, pos)
        tps = {}
        front = {}

        def transposes(j):
            tps[j] = []
            for lo in (0, 2):
                tp = ps_t.tile([P, 2, B, P], BF16, name="tp")
                for i in range(2):
                    hs, xs, tl = where[4 * j + lo + i]
                    for b in range(B):
                        nc.tensor.transpose(out=tp[:, i, b, :], in_=hs[:, b, tl, :], identity=perm[:])
                tps[j].append(tp)

        def regroup(j, q, copy=nc.scalar.copy):
            gi, pos = group_of[j]
            if pos == 0 and q == 0:
                grp = gpool.tile([P, 8, P * H], BF16, align_bytes=64, name="grp")
                front[gi] = {"grp": grp}
            lo = 4 * pos + 2 * q
            copy(
                out=front[gi]["grp"][:, lo : lo + 2, :].rearrange("p i c -> p (i c)").bitcast(F32),
                in_=tps[j][q][:].rearrange("p i b c -> p (i b c)").bitcast(F32),
            )

        def quantise(gi):
            n = 4 * len(GROUPS[gi])
            codes = gpool.tile([P, 8 * P], U32, align_bytes=64, name="codes")
            scl = gpool.tile([P, 8 * P], U8, align_bytes=64, name="scl")
            nc.vector.quantize_mx(
                out=codes[:, 0 : n * P].bitcast(FP8X4),
                scales=scl[:, 0 : n * P],
                in_=front[gi]["grp"][:, 0:n, :].rearrange("p i c -> p (i c)"),
            )
            front[gi]["codes"] = codes
            front[gi]["scl"] = scl

        def project(c):
            gi, pos = group_of[c]
            banks = []
            for i in range(4):
                j = 4 * pos + i
                o_ps = ps_o.tile([P, E], F32, name="o_ps")
                nc.tensor.matmul_mx(
                    out=o_ps[:],
                    lhsT=front[gi]["codes"][:, j * P : (j + 1) * P].bitcast(FP8X4),
                    lhsT_scale=front[gi]["scl"][:, j * P : (j + 1) * P],
                    rhs=w_codes[:].bitcast(FP8X4),
                    rhs_scale=w_scl[:],
                    start=True,
                    stop=True,
                )
                banks.append(o_ps)
            st[c] = {"o": banks}

        def ya(c, i):
            if c == 0:
                return st[c]["yg"][:, i, :]
            if i < 2:
                return st[c]["yv"][:, i, :]
            return st[c]["yg"][:, (i - 2 if c % 2 else i), :]

        def residual(c, lo=0, hi=4):
            if lo == 0:
                new_y(c)
            for i in range(lo, hi):
                hs, xs, tl = where[4 * c + i]
                nc.vector.scalar_tensor_tensor(
                    out=ya(c, i),
                    in0=st[c]["o"][i][:],
                    scalar=0.0,
                    in1=xs[:, tl, :],
                    op0=ALU.add,
                    op1=ALU.add,
                    accum_out=st[c]["sums"][:, i : i + 1],
                )

        def new_y(c):
            if c > 0:
                yv = yvpool.tile([P, 2, E], F32, name="yv")
                st[c]["yv"] = yv
            if c == 0 or c % 2:
                yg = ygpool.tile([P, 4, E], F32, name="yg")
                st[c]["yg"] = yg
            else:
                st[c]["yg"] = st[c - 1]["yg"]
            sums = small.tile([P, 4], F32, name="sums")
            st[c]["sums"] = sums

        def neg_mean(c, lo=0, hi=4):
            if lo == 0:
                nm = small.tile([P, 4], F32, name="nm")
                ssq = small.tile([P, 4], F32, name="ssq")
                rstd = small.tile([P, 4], F32, name="rstd")
                nmr = small.tile([P, 4], F32, name="nmr")
                st[c]["nm"] = nm
                st[c]["ssq"] = ssq
                st[c]["rstd"] = rstd
                st[c]["nmr"] = nmr
            nc.scalar.activation(out=st[c]["nm"][:, lo:hi], in_=st[c]["sums"][:, lo:hi], func=ACT.Copy, scale=-1.0 / E)

        def squares(c, tiles):
            for i in tiles:
                junk = jpool.tile([P, E], BF16, name="junk")
                nc.scalar.activation(
                    out=junk[:],
                    in_=ya(c, i),
                    func=ACT.Square,
                    bias=st[c]["nm"][:, i : i + 1],
                    scale=1.0,
                    accum_out=st[c]["ssq"][:, i : i + 1],
                )

        def inv_std(c, lo=0, hi=4):
            nc.scalar.activation(
                out=st[c]["rstd"][:, lo:hi],
                in_=st[c]["ssq"][:, lo:hi],
                func=ACT.Abs_reciprocal_sqrt,
                bias=eps[:, 0:1],
                scale=1.0 / E,
            )

        def centre_gamma(c, tiles=None):
            for i in on_vector(c) if tiles is None else tiles:
                nc.vector.scalar_tensor_tensor(
                    out=ya(c, i), in0=ya(c, i), scalar=st[c]["nm"][:, i : i + 1], in1=g_ps, op0=ALU.add, op1=ALU.mult
                )

        def scale_beta(c, tiles=None):
            for i in on_vector(c) if tiles is None else tiles:
                nc.vector.scalar_tensor_tensor(
                    out=ya(c, i), in0=ya(c, i), scalar=st[c]["rstd"][:, i : i + 1], in1=b_ps, op0=ALU.mult, op1=ALU.add
                )

        def shifts(c):
            for i in on_gpsimd(c)[-2:]:
                nc.scalar.activation(
                    out=st[c]["nmr"][:, i : i + 1],
                    in_=st[c]["nm"][:, i : i + 1],
                    func=ACT.Copy,
                    scale=st[c]["rstd"][:, i : i + 1],
                )

        def normalise(c, tiles=(2, 3)):
            for i in tiles:
                nc.scalar.activation(
                    out=ya(c, i),
                    in_=ya(c, i),
                    func=ACT.Identity,
                    bias=st[c]["nmr"][:, i : i + 1],
                    scale=st[c]["rstd"][:, i : i + 1],
                )

        def affine(c, n, lo=None):
            lo = lo if lo is not None else 0
            yg = st[c]["yg"][:, lo : lo + n, :]
            for vec, op in ((g_sb, ALU.mult), (b_sb, ALU.add)):
                nc.gpsimd.tensor_tensor(out=yg, in0=yg, in1=vec[:].unsqueeze(1).to_broadcast([P, n, E]), op=op)

        def store_v(c):
            if c > 0:
                nc.sync.dma_start(out=out_view[:, 4 * c : 4 * c + 2, :], in_=st[c]["yv"][:])

        def store_g(c):
            if c == 0:
                nc.sync.dma_start(out=out_view[:, 0:4, :], in_=st[c]["yg"][:])
                return
            lo = 0 if c % 2 else 2
            nc.sync.dma_start(out=out_view[:, 4 * c + 2 : 4 * c + 4, :], in_=st[c]["yg"][:, lo : lo + 2, :])

        transposes(0)
        regroup(0, 0)
        regroup(0, 1)

        w_grp = const.tile([P, E, H], BF16, align_bytes=64)
        nc.vector.tensor_copy(out=w_grp[:], in_=w_raw[:].rearrange("p h n -> p n h"))
        w_codes = const.tile([P, E], U32, align_bytes=64)
        w_scl = const.tile([P, E], U8, align_bytes=64)
        nc.vector.quantize_mx(
            out=w_codes[:].bitcast(FP8X4),
            scales=w_scl[:],
            in_=w_grp[:].rearrange("p n h -> p (n h)"),
        )

        gb_ps = ps_const.tile([P, 2, E], BF16)
        g_ps = gb_ps[:, 0, :]
        b_ps = gb_ps[:, 1, :]
        g_sb = const.tile([P, E], F32)
        b_sb = const.tile([P, E], F32)
        stores = {}

        for k in range(NCH - 1):
            if k in LOAD_AT:
                load(LOAD_AT[k])
            for c in stores.get(k, []):
                store_g(c)
            fb = [1, 2] if k == 0 else [k + 2] if k + 2 < NCH else []
            late = k >= 2 and k % 2 == 0
            if fb:
                transposes(fb[0])
            if k == 0:
                nc.tensor.matmul(out=g_ps, lhsT=ones[:], rhs=gb_row[:, 0:E], start=True, stop=True)
                nc.tensor.matmul(out=b_ps, lhsT=ones[:], rhs=gb_row[:, E : 2 * E], start=True, stop=True)
            if k < 2 or late:
                quantise(k if k < 2 else k // 2 + 1)
            project(k)
            if k >= 2:
                scale_beta(k - 2)
                store_v(k - 2)
            if k == 0:
                regroup(1, 0)
                regroup(1, 1, nc.vector.tensor_copy)
            if k == 1:
                regroup(2, 1, nc.vector.tensor_copy)
            if not late:
                residual(k)
            if fb and not late and k >= 3:
                regroup(fb[0], 0)
                regroup(fb[0], 1)
            if k >= 1:
                neg_mean(k - 1, 2 if k == 1 else 0)
            if k == 1:
                regroup(fb[0], 0)
            if k == 0:
                nc.scalar.copy(out=g_sb[:], in_=g_ps)
                nc.scalar.copy(out=b_sb[:], in_=b_ps)
            if k >= 2:
                normalise(k - 2)
            if late:
                if k == 2:
                    affine(0, 2, 2)
                else:
                    affine(k - 2, 4)
                stores[k + 2] = [0] if k == 2 else [k - 3, k - 2]
                squares(k - 1, [0, 1])
                centre_gamma(k - 1)
                if fb:
                    regroup(fb[0], 0)
                squares(k - 1, [2, 3])
                residual(k)
            elif k >= 3:
                squares(k - 1, [2, 3, 0])
                inv_std(k - 1, 2, 4)
                squares(k - 1, [1])
                shifts(k - 1)
                centre_gamma(k - 1)
            elif k == 1:
                squares(0, [2, 3])
                centre_gamma(0)
            if fb and (k == 1 or late):
                regroup(fb[0], 1)
            if k >= 3 and not late:
                inv_std(k - 1, 0, 2)
            elif k >= 1:
                inv_std(k - 1)
                shifts(k - 1)
            if k == 2:
                one = ya(0, 1)
                nc.gpsimd.tensor_scalar(
                    out=one,
                    in0=one,
                    scalar1=st[0]["nm"][:, 1:2],
                    scalar2=st[0]["rstd"][:, 1:2],
                    op0=ALU.add,
                    op1=ALU.mult,
                )
                affine(0, 1, 1)
            for j in fb[1:]:
                transposes(j)
                regroup(j, 0)
            if k == 0:
                neg_mean(0, 0, 2)
                squares(0, [0, 1])

        def store_rows(c, lo, hi):
            y = st[c]["yv"][:, lo:hi, :] if hi <= 2 else st[c]["yg"][:, (lo - 2 if c % 2 else lo) : (hi - 2 if c % 2 else hi), :]
            nc.sync.dma_start(out=out_view[:, 4 * c + lo : 4 * c + hi, :], in_=y)

        e = NCH - 1
        project(e)
        scale_beta(e - 2)
        store_v(e - 2)
        residual(e, 0, 2)
        neg_mean(e - 1)
        normalise(e - 2)
        affine(e - 2, 2)
        squares(e - 1, [0, 1, 2, 3])
        centre_gamma(e - 1)
        inv_std(e - 1)
        scale_beta(e - 1)
        for c in stores[e + 1]:
            store_g(c)
        store_rows(e - 1, 0, 2)
        store_rows(e - 1, 2, 4)
        residual(e, 2, 4)
        neg_mean(e, 0, 2)
        squares(e, [0, 1])
        centre_gamma(e, [0, 1])
        inv_std(e, 0, 2)
        neg_mean(e, 2, 4)
        squares(e, [2, 3])
        store_g(e - 2)
        scale_beta(e, [0, 1])
        store_rows(e, 0, 2)
        centre_gamma(e, [2, 3])
        inv_std(e, 2, 4)
        scale_beta(e, [2])
        store_rows(e, 2, 3)
        scale_beta(e, [3])
        store_rows(e, 3, 4)
